import numpy as np
import ml_dtypes


def mxq(x, axis, fmt="e4m3"):
    dtype, down = {"e4m3": (ml_dtypes.float8_e4m3fn, 7), "e5m2": (ml_dtypes.float8_e5m2, 14)}[fmt]
    v = np.moveaxis(np.asarray(x, np.float32).astype(ml_dtypes.bfloat16).astype(np.float64), axis, -1)
    blocks = v.reshape(v.shape[:-1] + (-1, 32))
    amax = np.abs(blocks).max(-1, keepdims=True)
    byte = np.maximum(np.where(amax > 0, np.frexp(amax)[1] - 1 + 127, 0) - down, 1)
    scale = np.exp2(byte - 127.0)
    codes = (blocks / scale).astype(np.float32).astype(dtype).astype(np.float64)
    return np.moveaxis((codes * scale).reshape(v.shape), -1, axis)


WIDE = False


def mx_kscale(k):
    if not WIDE:
        return np.ones(k)
    levels = np.array([10, -10, 5, -5, 0])
    if k % 512:
        return np.exp2(np.random.permutation(np.resize(levels, k // 32))).repeat(32)
    a = np.empty((k // 512, 16))
    for p in range(k // 512):
        a[p, :8] = np.random.permutation(np.resize(levels, 8))
        for g in range(8):
            far = levels[np.abs(levels - a[p, g]) >= 10]
            a[p, g + 8] = far[np.random.randint(len(far))]
    return np.exp2(a.ravel()).repeat(32)


BF16 = ml_dtypes.bfloat16


def bf(x):
    return np.asarray(x, np.float32).astype(BF16)


def f64(x):
    return np.asarray(x).astype(np.float64)


B, T, HID, H, NOPE, ROPE, VD, KV_LORA = 1, 512, 2048, 16, 64, 128, 128, 512
HALF = ROPE // 2
EPS = 1e-5


def rope(x, cos, sin):
    c = cos[None, :, None, :]
    s = sin[None, :, None, :]
    x1, x2 = x[..., 0::2], x[..., 1::2]
    o1 = x1 * c - x2 * s
    o2 = x1 * s + x2 * c
    return np.stack([o1, o2], axis=-1).reshape(x.shape)


def layernorm(x, g, b):
    mu = x.mean(-1, keepdims=True)
    var = x.var(-1, keepdims=True)
    return (x - mu) / np.sqrt(var + EPS) * g + b


def draw0():
    s, t = mx_kscale(HID), mx_kscale(KV_LORA)
    ang = np.random.uniform(-np.pi, np.pi, (T, HALF))
    return {"hidden_states": bf(np.random.standard_normal((B, T, HID)) * s),
            "rope_cos": bf(np.cos(ang)), "rope_sin": bf(np.sin(ang)),
            "Wkv_a": bf(np.random.standard_normal((HID, KV_LORA + ROPE)) / np.sqrt(HID) / s[:, None]),
            "kv_gamma": bf((1.0 + 0.1 * np.random.standard_normal(KV_LORA)) * t),
            "kv_beta": bf(0.1 * np.random.standard_normal(KV_LORA) * t),
            "Wkv_b": bf(np.random.standard_normal((KV_LORA, H * (NOPE + VD))) / np.sqrt(KV_LORA) / t[:, None])}


def core(hidden_states, rope_cos, rope_sin, Wkv_a, kv_gamma, kv_beta, Wkv_b):
    kv = mxq(f64(hidden_states), 2, "e4m3") @ mxq(f64(Wkv_a), 0, "e4m3")
    kv_lat, k_rope = kv[..., :KV_LORA], kv[..., KV_LORA:]
    k_rope = rope(k_rope[:, :, None, :], f64(rope_cos), f64(rope_sin))
    kv_lat = layernorm(kv_lat, f64(kv_gamma), f64(kv_beta))
    kvb = (mxq(kv_lat, 2, "e4m3") @ mxq(f64(Wkv_b), 0, "e4m3")).reshape(B, T, H, NOPE + VD)
    k_nope, v = kvb[..., :NOPE], kvb[..., NOPE:]
    k = np.concatenate([k_nope, np.broadcast_to(k_rope, (B, T, H, ROPE))], axis=-1)
    return k, v


def e4m3fn_bytes(y):
    return np.clip(np.asarray(y, np.float64), -448.0, 448.0).astype(np.float32).astype(ml_dtypes.float8_e4m3fn).view(np.uint8)


def e4m3fn_values(b):
    return np.asarray(b, np.uint8).view(ml_dtypes.float8_e4m3fn).astype(np.float64)


def setup_inputs():
    d = draw0()
    x0 = np.asarray(d['Wkv_b']).astype(np.float64)
    s = (np.max(np.abs(x0), axis=(1,), keepdims=True) / 448.0).astype(np.float32)
    out = {}
    for k, v in d.items():
        if k == 'Wkv_b':
            out['Wkv_b_bytes'] = e4m3fn_bytes(x0 / s.astype(np.float64))
            out['Wkv_b_scale'] = s
        else:
            out[k] = v
    return out


def reference(hidden_states, rope_cos, rope_sin, Wkv_a, kv_gamma, kv_beta, Wkv_b_bytes, Wkv_b_scale):
    return core(hidden_states, rope_cos, rope_sin, Wkv_a, kv_gamma, kv_beta, e4m3fn_values(Wkv_b_bytes) * Wkv_b_scale.astype(np.float64))

@@ -1,0 +1,511 @@
+from contextlib import ExitStack
+
+import concourse.mybir as mybir
+from concourse.masks import make_identity
+
+T, HID, H, NOPE, ROPE, VD, LAT = 512, 2048, 16, 64, 128, 128, 512
+HALF = ROPE // 2
+KV = LAT + ROPE
+HEAD = NOPE + VD
+EPS = 1e-5
+
+FLOPS = 2 * T * HID * KV + 2 * T * LAT * H * HEAD
+
+F32 = mybir.dt.float32
+BF16 = mybir.dt.bfloat16
+U32 = mybir.dt.uint32
+U8 = mybir.dt.uint8
+FP8 = mybir.dt.float8_e4m3fn
+FP8X4 = mybir.dt.float8_e4m3fn_x4
+ALU = mybir.AluOpType
+ACT = mybir.ActivationFunctionType
+
+P = 128
+PACK = 4
+NG = HID // (P * PACK)
+NT = T // P
+GH = 4
+NHG = H // GH
+GC = GH * HEAD
+GV = GH * VD
+GN = GH * NOPE
+S_COL = 480
+
+
+def tile_multilatentattention_pa_kernel(
+    tc, hidden_states, rope_cos, rope_sin, wkv_a, kv_gamma, kv_beta, wkv_b_bytes, wkv_b_scale, out_k, out_v
+):
+    nc = tc.nc
+    with ExitStack() as ctx:
+        one = ctx.enter_context(tc.tile_pool(name="one", bufs=1))
+        work = ctx.enter_context(tc.tile_pool(name="work", bufs=2))
+        psum = ctx.enter_context(tc.psum_pool(name="psum", bufs=8))
+
+        hid_v = hidden_states.rearrange("b (p i) k -> i p (b k)", i=NT)
+        cos_v = rope_cos.rearrange("(p i) c -> p i c", i=NT)
+        sin_v = rope_sin.rearrange("(p i) c -> p i c", i=NT)
+        wa_v = wkv_a.rearrange("(g p t) w -> g p t w", p=P, t=PACK)
+        wb_v = wkv_b_bytes.rearrange("(p t) n -> p t n", t=PACK)
+        scale_v = wkv_b_scale.rearrange("(p t) o -> p (t o)", t=PACK)
+        k_v = out_k.rearrange("b (p i) h c -> i p (b h) c", i=NT)
+        v_v = out_v.rearrange("b (p i) h c -> i p (b h c)", i=NT)
+
+        ident = one.tile([P, P], F32, name="ident", align_bytes=64)
+        make_identity(nc, ident[:])
+        neg_half = one.tile([P, 1], F32, name="neg_half")
+        nc.gpsimd.memset(neg_half[:], -0.5)
+        gb_rows = one.tile([P, 2 * LAT], BF16, name="gb_rows", align_bytes=64)
+        nc.vector.memset(gb_rows[:], 0.0)
+        ones = one.tile([P, P], BF16, name="ones", align_bytes=64)
+        nc.vector.memset(ones[:], 1.0)
+
+        wb_scale = one.tile([P, PACK], F32, name="wb_scale")
+        nc.scalar.dma_start(out=wb_scale[:], in_=scale_v)
+        wa_raw = [one.tile([P, PACK, KV], BF16, name=f"wa_raw{g}", align_bytes=64) for g in range(NG)]
+        hid = [one.tile([P, HID], BF16, name=f"hid{i}", align_bytes=64) for i in range(NT)]
+        wb_bytes = [one.tile([P, PACK, GC], U8, name=f"wb_bytes{q}", align_bytes=64) for q in range(NHG)]
+        cos = one.tile([P, NT, HALF], BF16, name="cos")
+        sin = one.tile([P, NT, HALF], BF16, name="sin")
+
+        def load_wa(g, a=0, b=KV):
+            nc.sync.dma_start(out=wa_raw[g][:, :, a:b], in_=wa_v[g][:, :, a:b])
+
+        def load_hid(i):
+            nc.sync.dma_start(out=hid[i][:], in_=hid_v[i])
+
+        def load_wb(q, t0=0, t1=PACK):
+            nc.sync.dma_start(out=wb_bytes[q][:, t0:t1], in_=wb_v[:, t0:t1, q * GC : (q + 1) * GC])
+
+        def load_gb():
+            nc.sync.dma_start(out=gb_rows[0:1, 0:LAT], in_=kv_gamma.rearrange("(o c) -> o c", o=1))
+            nc.sync.dma_start(out=gb_rows[0:1, LAT:], in_=kv_beta.rearrange("(o c) -> o c", o=1))
+
+        def load_rot():
+            nc.sync.dma_start(out=cos[:], in_=cos_v)
+            nc.sync.dma_start(out=sin[:], in_=sin_v)
+
+        def empty(out, in_, engine):
+            if engine == "s":
+                nc.scalar.copy(out=out, in_=in_)
+            else:
+                nc.vector.tensor_copy(out=out, in_=in_)
+
+        gamma = one.tile([P, LAT], BF16, name="gamma", align_bytes=64)
+        beta = one.tile([P, LAT], BF16, name="beta", align_bytes=64)
+
+        def spread(j, engine):
+            dst = (gamma, beta)[j]
+            bank = psum.tile([P, 512], F32, name="bank", tag="bank")
+            nc.tensor.matmul(bank[:], lhsT=ones[:], rhs=gb_rows[:, j * LAT : (j + 1) * LAT], start=True, stop=True)
+            empty(dst[:], bank[:], engine)
+
+        sgn_sin = one.tile([P, NT, HALF, 2], BF16, name="sgn_sin")
+
+        def signed_sin():
+            for j, sign in enumerate((-1.0, 1.0)):
+                nc.gpsimd.tensor_scalar(
+                    out=sgn_sin[:, :, :, j], in0=sin[:], scalar1=sign, scalar2=0.0, op0=ALU.mult, op1=ALU.add
+                )
+
+        wa_codes = [one.tile([P, KV], U32, name=f"wa_codes{g}", align_bytes=64) for g in range(NG)]
+        wa_scales = [one.tile([P, KV], U8, name=f"wa_scales{g}", align_bytes=64) for g in range(NG)]
+        hid_codes = [one.tile([P, NG * P], U32, name=f"hid_codes{i}", align_bytes=64) for i in range(NT)]
+        hid_scales = [one.tile([P, NG * P], U8, name=f"hid_scales{i}", align_bytes=64) for i in range(NT)]
+
+        wa_grouped = [one.tile([P, KV, PACK], BF16, name=f"wa_grouped{g}", align_bytes=64) for g in range(NG)]
+
+        def wa_i(g, a, b, engine):
+            dst = wa_grouped[g][:, a:b, :].rearrange("p (c i) t -> p c t i", i=4)
+            src = wa_raw[g][:, :, a:b].rearrange("p t (c i) -> p c t i", i=4)
+            if engine == "v":
+                nc.vector.tensor_copy(out=dst, in_=src)
+            else:
+                nc.scalar.copy(out=dst, in_=src)
+
+        def wa_q(g):
+            flat = wa_grouped[g][:].rearrange("p c t -> p (c t)")
+            for a, b in ((0, LAT), (LAT, KV)):
+                nc.vector.quantize_mx(
+                    out=wa_codes[g][:, a:b].bitcast(FP8X4), scales=wa_scales[g][:, a:b], in_=flat[:, a * PACK : b * PACK]
+                )
+
+        hid_grouped = [one.tile([P, NG * P * PACK], BF16, name=f"hid_grouped{i}", align_bytes=64) for i in range(NT)]
+
+        hid_bank = {}
+
+        def hid_t(i, half):
+            words = hid[i][:].bitcast(F32)
+            xt = psum.tile([P, 2, 2, P], F32, name="bank", tag="bank")
+            for gg in range(2):
+                g = 2 * half + gg
+                for u in range(2):
+                    nc.tensor.transpose(xt[:, gg, u, :], words[:, 256 * g + u : 256 * (g + 1) : 2], ident[:])
+            hid_bank[i, half] = xt
+
+        def hid_c(i, half, engine):
+            out = hid_grouped[i][:, half * 1024 : (half + 1) * 1024].bitcast(F32).rearrange("p (g r u) -> p g r u", g=2, u=2)
+            empty(out, hid_bank[i, half][:].rearrange("p g u r -> p g r u"), engine)
+
+        def hid_q(i):
+            nc.vector.quantize_mx(out=hid_codes[i][:].bitcast(FP8X4), scales=hid_scales[i][:], in_=hid_grouped[i][:])
+
+        kv = {}
+        rp = {}
+
+        def mm1(i, g):
+            if g == 0:
+                kv[i] = psum.tile([P, LAT], F32, name="bank", tag="bank")
+                rp[i] = psum.tile([P, 512], F32, name="bank", tag="bank")
+            toks = slice(g * P, (g + 1) * P)
+            for dst, a, b in ((kv[i][:], 0, LAT), (rp[i][:, 0:ROPE], LAT, KV)):
+                nc.tensor.matmul_mx(
+                    out=dst,
+                    lhsT=hid_codes[i][:, toks].bitcast(FP8X4),
+                    lhsT_scale=hid_scales[i][:, toks],
+                    rhs=wa_codes[g][:, a:b].bitcast(FP8X4),
+                    rhs_scale=wa_scales[g][:, a:b],
+                    start=(g == 0),
+                    stop=(g == NG - 1),
+                )
+
+        lat = {}
+        k_sb = [one.tile([P, 2 * GH, NOPE + ROPE], F32, name=f"k_sb{i}", align_bytes=64) for i in range(NT)]
+
+        mvs = {}
+        rstds = {}
+        cens = {}
+
+        def bn(i):
+            stats = work.tile([P, 6], F32, name="stats", bufs=4)
+            nc.vector.bn_stats(out=stats[:], in_=kv[i][:])
+            mv = work.tile([P, 2], F32, name="mv", bufs=4)
+            nc.vector.bn_aggr(out=mv[:], in_=stats[:])
+            ve = work.tile([P, 1], F32, name="ve", bufs=4)
+            rstd = work.tile([P, 1], F32, name="rstd", bufs=4)
+            nc.gpsimd.tensor_scalar(out=ve[:], in0=mv[:, 1:2], scalar1=EPS, scalar2=None, op0=ALU.add)
+            nc.gpsimd.tensor_tensor(out=rstd[:], in0=ve[:], in1=neg_half[:], op=ALU.pow)
+            mvs[i] = mv
+            rstds[i] = rstd
+
+        def cen(i):
+            cens[i] = work.tile([P, LAT], F32, name="cen", bufs=4)
+            nc.vector.scalar_tensor_tensor(
+                out=cens[i][:], in0=kv[i][:], scalar=mvs[i][:, 0:1], in1=gamma[:], op0=ALU.subtract, op1=ALU.mult
+            )
+
+        def fin(i):
+            lat[i] = work.tile([P, LAT], BF16, name="lat", bufs=4, align_bytes=64)
+            nc.vector.scalar_tensor_tensor(
+                out=lat[i][:], in0=cens[i][:], scalar=rstds[i][:], in1=beta[:], op0=ALU.mult, op1=ALU.add
+            )
+
+        rots = {}
+
+        def rope_a(i):
+            x = rp[i][:, 0:ROPE].rearrange("p (c two) -> p c two", two=2)
+            xc = work.tile([P, HALF, 2], F32, name="xc", bufs=4)
+            xs = work.tile([P, HALF, 2], F32, name="xs", bufs=4)
+            rots[i] = (xc, xs)
+            c2 = cos[:, i, :].unsqueeze(2).to_broadcast([P, HALF, 2])
+            nc.vector.tensor_tensor(out=xc[:], in0=x, in1=c2, op=ALU.mult)
+            nc.vector.tensor_tensor(out=xs[:], in0=x[:, :, ::-1], in1=sgn_sin[:, i], op=ALU.mult)
+
+        def rope_b(i):
+            xc, xs = rots[i]
+            r = work.tile([P, ROPE], F32, name="r", bufs=4)
+            nc.vector.tensor_tensor(
+                out=r[:].rearrange("p (c two) -> p c two", two=2), in0=xc[:], in1=xs[:], op=ALU.add
+            )
+            rots[i] = r
+
+        def rope_r(i):
+            nc.vector.tensor_copy(
+                out=k_sb[i][:, :, NOPE:], in_=rots[i][:].unsqueeze(1).to_broadcast([P, 2 * GH, ROPE])
+            )
+
+        lat_codes = [one.tile([P, P], U32, name=f"lat_codes{i}", align_bytes=64) for i in range(NT)]
+        lat_scales = [one.tile([P, P], U8, name=f"lat_scales{i}", align_bytes=64) for i in range(NT)]
+
+        lat_grouped = [one.tile([P, P * PACK], BF16, name=f"lat_grouped{i}", align_bytes=64) for i in range(NT)]
+
+        lat_bank = {}
+
+        def lat_t(i):
+            words = lat[i][:].bitcast(F32)
+            xt = psum.tile([P, 4, P], F32, name="bank", tag="bank")
+            for u in range(2):
+                nc.tensor.transpose(xt[:, u, :], words[:, u::2], ident[:])
+            lat_bank[i] = xt
+
+        def lat_c(i, engine):
+            out = lat_grouped[i][:].bitcast(F32).rearrange("p (r u) -> p r u", u=2)
+            empty(out, lat_bank[i][:, 0:2, :].rearrange("p u r -> p r u"), engine)
+
+        def lat_q(i):
+            nc.vector.quantize_mx(out=lat_codes[i][:].bitcast(FP8X4), scales=lat_scales[i][:], in_=lat_grouped[i][:])
+
+        v_codes = [one.tile([P, GV], U32, name=f"v_codes{q}", align_bytes=64) for q in range(NHG)]
+        v_scales = [one.tile([P, GV], U8, name=f"v_scales{q}", align_bytes=64) for q in range(NHG)]
+        n_codes = [one.tile([P, 2 * GN], U32, name=f"n_codes{h}", align_bytes=64) for h in range(NHG // 2)]
+        n_scales = [one.tile([P, 2 * GN], U8, name=f"n_scales{h}", align_bytes=64) for h in range(NHG // 2)]
+
+        wide = {}
+        gvs = {}
+        gns = {}
+
+        def wb_w(q, ts=(0, 1, 2, 3), engine="s"):
+            if q not in wide:
+                wide[q] = work.tile([P, PACK, GC], BF16, name="wb_wide", bufs=4, align_bytes=64)
+            for t in ts:
+                raw = wb_bytes[q][:, t, :].bitcast(FP8)
+                if engine == "s":
+                    nc.scalar.activation(out=wide[q][:, t, :], in_=raw, func=ACT.Copy, scale=wb_scale[:, t : t + 1])
+                else:
+                    nc.vector.tensor_scalar(
+                        out=wide[q][:, t, :], in0=raw, scalar1=wb_scale[:, t : t + 1], scalar2=None, op0=ALU.mult
+                    )
+
+        def wb_iv(q):
+            heads = wide[q][:].rearrange("p t (h c) -> p h c t", h=GH)
+            gvs[q] = work.tile([P, GH, VD, PACK], BF16, name="wb_gv", align_bytes=64)
+            nc.vector.tensor_copy(out=gvs[q][:], in_=heads[:, :, NOPE:, :])
+
+        def wb_in(q):
+            heads = wide[q][:].rearrange("p t (h c) -> p h c t", h=GH)
+            gns[q] = work.tile([P, GH, NOPE, PACK], BF16, name="wb_gn", align_bytes=64)
+            nc.vector.tensor_copy(out=gns[q][:], in_=heads[:, :, :NOPE, :])
+
+        def wb_qv(q):
+            nc.vector.quantize_mx(
+                out=v_codes[q][:].bitcast(FP8X4), scales=v_scales[q][:], in_=gvs[q][:].rearrange("p h c t -> p (h c t)")
+            )
+
+        def wb_qn(q):
+            cols = slice((q % 2) * GN, (q % 2 + 1) * GN)
+            nc.vector.quantize_mx(
+                out=n_codes[q // 2][:, cols].bitcast(FP8X4),
+                scales=n_scales[q // 2][:, cols],
+                in_=gns[q][:].rearrange("p h c t -> p (h c t)"),
+            )
+
+        banks = {}
+
+        def mm2(key, i, codes, scales):
+            bank = psum.tile([P, 512], F32, name="bank", tag="bank")
+            nc.tensor.matmul_mx(
+                out=bank[:],
+                lhsT=lat_codes[i][:].bitcast(FP8X4),
+                lhsT_scale=lat_scales[i][:],
+                rhs=codes[:].bitcast(FP8X4),
+                rhs_scale=scales[:],
+                start=True,
+                stop=True,
+            )
+            banks[key] = bank
+
+        def mv(i, q):
+            mm2(("v", i, q), i, v_codes[q], v_scales[q])
+
+        def mk(i, h):
+            mm2(("k", i, h), i, n_codes[h], n_scales[h])
+
+        def ov(i, q, engine):
+            v_sb = work.tile([P, GV], F32, name="v_sb", bufs=8)
+            empty(v_sb[:], banks["v", i, q][:], engine)
+            nc.sync.dma_start(out=v_v[i][:, q * GV : (q + 1) * GV], in_=v_sb[:])
+
+        def ok(i, h, engine):
+            empty(k_sb[i][:, :, :NOPE], banks["k", i, h][:].rearrange("p (h c) -> p h c", c=NOPE), engine)
+            nc.sync.dma_start(out=k_v[i][:, 2 * GH * h : 2 * GH * (h + 1), :], in_=k_sb[i][:])
+
+        with tc.manual_schedule():
+            load_wb(0)
+            wb_w(0, (0,), "s")
+            wb_w(0, (2,), "v")
+            wb_w(0, (1,), "v")
+            load_wb(1)
+            load_gb()
+            wb_w(1, (1,), "s")
+            load_wa(2)
+            wb_w(1, (3,), "s")
+            wa_i(2, 480, 640, "s")
+            spread(1, "s")
+            wb_w(1, (2,), "v")
+            wb_w(0, (3,), "v")
+            load_wa(1)
+            load_wa(0, 320, KV)
+            wb_w(1, (0,), "v")
+            wb_in(0)
+            wa_i(2, 320, 480, "v")
+            load_hid(2)
+            wb_iv(0)
+            load_hid(3)
+            hid_t(2, 0)
+            wa_i(1, 480, 640, "v")
+            wb_iv(1)
+            load_wa(0, 0, 320)
+            wa_i(1, 320, 480, "s")
+            wa_i(1, 160, 320, "v")
+            load_hid(0)
+            wb_in(1)
+            wa_i(0, 0, 160, "v")
+            load_wa(3)
+            hid_t(2, 1)
+            wa_i(0, 320, 480, "s")
+            wa_i(2, 0, 160, "s")
+            wa_i(0, 480, 640, "s")
+            wa_i(1, 0, 160, "s")
+            hid_t(3, 0)
+            load_wb(3)
+            hid_c(3, 0, "s")
+            wa_q(1)
+            hid_t(3, 1)
+            load_rot()
+            wa_i(0, 160, 320, "v")
+            hid_c(3, 1, "s")
+            signed_sin()
+            hid_q(3)
+            hid_c(2, 0, "s")
+            wa_i(2, 160, 320, "v")
+            load_wb(2)
+            hid_t(0, 0)
+            hid_t(0, 1)
+            hid_c(0, 0, "s")
+            wa_i(3, 320, 480, "s")
+            wa_q(0)
+            mm1(3, 0)
+            mm1(3, 1)
+            wa_i(3, 480, 640, "s")
+            wa_i(3, 0, 160, "v")
+            wb_qn(1)
+            wa_q(2)
+            load_hid(1)
+            wa_i(3, 160, 320, "s")
+            wa_q(3)
+            hid_c(2, 1, "s")
+            hid_q(2)
+            hid_c(0, 1, "s")
+            spread(0, "s")
+            mm1(3, 2)
+            mm1(3, 3)
+            wb_w(3, (2,), "s")
+            wb_w(2, (3,), "s")
+            wb_w(2, (0,), "s")
+            hid_q(0)
+            bn(3)
+            rope_a(3)
+            cen(3)
+            mm1(2, 0)
+            mm1(2, 1)
+            mm1(2, 2)
+            mm1(2, 3)
+            wb_qn(0)
+            wb_w(3, (3,), "s")
+            fin(3)
+            mm1(0, 0)
+            wb_qv(1)
+            hid_t(1, 0)
+            lat_t(3)
+            bn(2)
+            wb_w(3, (0,), "s")
+            lat_c(3, "s")
+            mm1(0, 1)
+            mm1(0, 2)
+            lat_q(3)
+            rope_b(3)
+            wb_w(3, (1,), "s")
+            hid_c(1, 0, "s")
+            mv(3, 1)
+            ov(3, 1, "s")
+            mk(3, 0)
+            cen(2)
+            rope_r(3)
+            fin(2)
+            hid_t(1, 1)
+            ok(3, 0, "s")
+            lat_t(2)
+            hid_c(1, 1, "s")
+            wb_qv(0)
+            lat_c(2, "s")
+            rope_a(2)
+            wb_in(3)
+            mv(3, 0)
+            lat_q(2)
+            rope_b(2)
+            wb_w(2, (2,), "s")
+            mm1(0, 3)
+            ov(3, 0, "s")
+            mk(2, 0)
+            hid_q(1)
+            wb_w(2, (1,), "s")
+            rope_r(2)
+            bn(0)
+            ok(2, 0, "s")
+            wb_in(2)
+            wb_qn(3)
+            mv(2, 1)
+            wb_qn(2)
+            cen(0)
+            mm1(1, 0)
+            mm1(1, 1)
+            mm1(1, 2)
+            fin(0)
+            mv(2, 0)
+            mm1(1, 3)
+            ov(2, 1, "s")
+            ov(2, 0, "s")
+            mk(3, 1)
+            ok(3, 1, "s")
+            mk(2, 1)
+            ok(2, 1, "s")
+            lat_t(0)
+            bn(1)
+            lat_c(0, "s")
+            rope_a(0)
+            lat_q(0)
+            mv(0, 0)
+            cen(1)
+            mk(0, 0)
+            rope_b(0)
+            fin(1)
+            lat_t(1)
+            ov(0, 0, "s")
+            rope_r(0)
+            ok(0, 0, "s")
+            rope_a(1)
+            lat_c(1, "s")
+            lat_q(1)
+            rope_b(1)
+            rope_r(1)
+            mv(0, 1)
+            mk(1, 0)
+            wb_iv(3)
+            ov(0, 1, "s")
+            mv(1, 1)
+            mk(1, 1)
+            wb_iv(2)
+            ok(1, 0, "s")
+            mk(0, 1)
+            ok(0, 1, "s")
+            ov(1, 1, "s")
+            wb_qv(2)
+            wb_qv(3)
+            mv(1, 0)
+            mv(1, 2)
+            mv(3, 3)
+            mv(2, 3)
+            ok(1, 1, "s")
+            mv(2, 2)
+            mv(0, 2)
+            ov(1, 2, "s")
+            mv(0, 3)
+            ov(1, 0, "s")
+            ov(2, 2, "v")
+            mv(1, 3)
+            ov(0, 2, "s")
+            ov(2, 3, "v")
+            mv(3, 2)
+            ov(3, 2, "s")
+            ov(1, 3, "s")
+            ov(3, 3, "v")
+            ov(0, 3, "s")

@@ -52,6 +52,8 @@ def tile_multilatentattention_pa_kernel(
 
         ident = one.tile([P, P], F32, name="ident", align_bytes=64)
         make_identity(nc, ident[:])
+        ident_bf = one.tile([P, P], BF16, name="ident_bf", align_bytes=64)
+        make_identity(nc, ident_bf[:])
         neg_half = one.tile([P, 1], F32, name="neg_half")
         nc.gpsimd.memset(neg_half[:], -0.5)
         gb_rows = one.tile([P, 2 * LAT], BF16, name="gb_rows", align_bytes=64)
@@ -63,7 +65,7 @@ def tile_multilatentattention_pa_kernel(
         nc.scalar.dma_start(out=wb_scale[:], in_=scale_v)
         wa_raw = [one.tile([P, PACK, KV], BF16, name=f"wa_raw{g}", align_bytes=64) for g in range(NG)]
         hid = [one.tile([P, HID], BF16, name=f"hid{i}", align_bytes=64) for i in range(NT)]
-        wb_bytes = [one.tile([P, PACK, GC], U8, name=f"wb_bytes{q}", align_bytes=64) for q in range(NHG)]
+        wb_bytes = [one.tile([P, NHG * GC], U8, name=f"wb_bytes{t}", align_bytes=64) for t in range(PACK)]
         cos = one.tile([P, NT, HALF], BF16, name="cos")
         sin = one.tile([P, NT, HALF], BF16, name="sin")
 
@@ -73,8 +75,9 @@ def tile_multilatentattention_pa_kernel(
         def load_hid(i):
             nc.sync.dma_start(out=hid[i][:], in_=hid_v[i])
 
-        def load_wb(q, t0=0, t1=PACK):
-            nc.sync.dma_start(out=wb_bytes[q][:, t0:t1], in_=wb_v[:, t0:t1, q * GC : (q + 1) * GC])
+        def load_wb(t, a=0, b=NHG):
+            cols = slice(a * GC, b * GC)
+            nc.sync.dma_start(out=wb_bytes[t][:, cols], in_=wb_v[:, t, cols])
 
         def load_gb():
             nc.sync.dma_start(out=gb_rows[0:1, 0:LAT], in_=kv_gamma.rearrange("(o c) -> o c", o=1))
@@ -90,14 +93,20 @@ def tile_multilatentattention_pa_kernel(
             else:
                 nc.vector.tensor_copy(out=out, in_=in_)
 
-        gamma = one.tile([P, LAT], BF16, name="gamma", align_bytes=64)
-        beta = one.tile([P, LAT], BF16, name="beta", align_bytes=64)
+        gamma_beta = one.tile([P, 2 * LAT], BF16, name="gamma_beta", align_bytes=64)
+        gamma = gamma_beta[:, 0:LAT]
+        beta = gamma_beta[:, LAT:]
+        spread_bank = {}
 
-        def spread(j, engine):
-            dst = (gamma, beta)[j]
-            bank = psum.tile([P, 512], F32, name="bank", tag="bank")
-            nc.tensor.matmul(bank[:], lhsT=ones[:], rhs=gb_rows[:, j * LAT : (j + 1) * LAT], start=True, stop=True)
-            empty(dst[:], bank[:], engine)
+        def spread_m():
+            bank = psum.tile([P, 2 * LAT], BF16, name="bank", tag="bank")
+            for j in range(2):
+                half = slice(j * LAT, (j + 1) * LAT)
+                nc.tensor.matmul(bank[:, half], lhsT=ones[:], rhs=gb_rows[:, half], start=True, stop=True)
+            spread_bank[0] = bank
+
+        def spread_c(engine):
+            empty(gamma_beta[:], spread_bank[0][:], engine)
 
         sgn_sin = one.tile([P, NT, HALF, 2], BF16, name="sgn_sin")
 
@@ -121,6 +130,25 @@ def tile_multilatentattention_pa_kernel(
                 nc.vector.tensor_copy(out=dst, in_=src)
             else:
                 nc.scalar.copy(out=dst, in_=src)
+
+        wa_bank = {}
+
+        def wa_m(g, j):
+            bank = psum.tile([P, 256, PACK], BF16, name="bank", tag="bank")
+            for m in range(2):
+                c0 = 256 * j + P * m
+                nc.tensor.matmul(
+                    bank[:, P * m : P * (m + 1), :],
+                    lhsT=ident_bf[:],
+                    rhs=wa_raw[g][:, :, c0 : c0 + P].rearrange("p t c -> p c t"),
+                    start=True,
+                    stop=True,
+                )
+            wa_bank[g, j] = bank
+
+        def wa_e(g, j, engine):
+            out = wa_grouped[g][:, 256 * j : 256 * (j + 1), :].rearrange("p c t -> p (c t)")
+            empty(out, wa_bank[g, j][:].rearrange("p c t -> p (c t)"), engine)
 
         def wa_q(g):
             flat = wa_grouped[g][:].rearrange("p c t -> p (c t)")
@@ -169,17 +197,25 @@ def tile_multilatentattention_pa_kernel(
                 )
 
         lat = {}
-        k_sb = [one.tile([P, 2 * GH, NOPE + ROPE], F32, name=f"k_sb{i}", align_bytes=64) for i in range(NT)]
+        k_sb = {(i, 0): one.tile([P, 2 * GH, NOPE + ROPE], F32, name=f"k_sb{i}", align_bytes=64) for i in range(NT)}
+        for i in range(NT - 1):
+            k_sb[i, 1] = k_sb[i, 0]
+        k_sb[NT - 1, 1] = one.tile([P, 2 * GH, NOPE + ROPE], F32, name="k_sb_last", align_bytes=64)
 
         mvs = {}
         rstds = {}
         cens = {}
 
-        def bn(i):
-            stats = work.tile([P, 6], F32, name="stats", bufs=4)
-            nc.vector.bn_stats(out=stats[:], in_=kv[i][:])
+        stats = {}
+
+        def bn_s(i):
+            stat = work.tile([P, 6], F32, name="stat", bufs=4)
+            nc.vector.bn_stats(out=stat[:], in_=kv[i][:])
+            stats[i] = stat
+
+        def bn_a(i):
             mv = work.tile([P, 2], F32, name="mv", bufs=4)
-            nc.vector.bn_aggr(out=mv[:], in_=stats[:])
+            nc.vector.bn_aggr(out=mv[:], in_=stats[i][:])
             ve = work.tile([P, 1], F32, name="ve", bufs=4)
             rstd = work.tile([P, 1], F32, name="rstd", bufs=4)
             nc.gpsimd.tensor_scalar(out=ve[:], in0=mv[:, 1:2], scalar1=EPS, scalar2=None, op0=ALU.add)
@@ -188,23 +224,23 @@ def tile_multilatentattention_pa_kernel(
             rstds[i] = rstd
 
         def cen(i):
-            cens[i] = work.tile([P, LAT], F32, name="cen", bufs=4)
+            cens[i] = work.tile([P, LAT], F32, name="cen", bufs=2)
             nc.vector.scalar_tensor_tensor(
-                out=cens[i][:], in0=kv[i][:], scalar=mvs[i][:, 0:1], in1=gamma[:], op0=ALU.subtract, op1=ALU.mult
+                out=cens[i][:], in0=kv[i][:], scalar=mvs[i][:, 0:1], in1=gamma, op0=ALU.subtract, op1=ALU.mult
             )
 
         def fin(i):
             lat[i] = work.tile([P, LAT], BF16, name="lat", bufs=4, align_bytes=64)
             nc.vector.scalar_tensor_tensor(
-                out=lat[i][:], in0=cens[i][:], scalar=rstds[i][:], in1=beta[:], op0=ALU.mult, op1=ALU.add
+                out=lat[i][:], in0=cens[i][:], scalar=rstds[i][:], in1=beta, op0=ALU.mult, op1=ALU.add
             )
 
         rots = {}
 
         def rope_a(i):
             x = rp[i][:, 0:ROPE].rearrange("p (c two) -> p c two", two=2)
-            xc = work.tile([P, HALF, 2], F32, name="xc", bufs=4)
-            xs = work.tile([P, HALF, 2], F32, name="xs", bufs=4)
+            xc = work.tile([P, HALF, 2], F32, name="xc", bufs=2)
+            xs = work.tile([P, HALF, 2], F32, name="xs", bufs=2)
             rots[i] = (xc, xs)
             c2 = cos[:, i, :].unsqueeze(2).to_broadcast([P, HALF, 2])
             nc.vector.tensor_tensor(out=xc[:], in0=x, in1=c2, op=ALU.mult)
@@ -213,15 +249,13 @@ def tile_multilatentattention_pa_kernel(
         def rope_b(i):
             xc, xs = rots[i]
             r = work.tile([P, ROPE], F32, name="r", bufs=4)
-            nc.vector.tensor_tensor(
+            nc.gpsimd.tensor_tensor(
                 out=r[:].rearrange("p (c two) -> p c two", two=2), in0=xc[:], in1=xs[:], op=ALU.add
             )
             rots[i] = r
 
-        def rope_r(i):
-            nc.vector.tensor_copy(
-                out=k_sb[i][:, :, NOPE:], in_=rots[i][:].unsqueeze(1).to_broadcast([P, 2 * GH, ROPE])
-            )
+        def rope_r(i, h, engine):
+            empty(k_sb[i, h][:, :, NOPE:], rots[i][:].unsqueeze(1).to_broadcast([P, 2 * GH, ROPE]), engine)
 
         lat_codes = [one.tile([P, P], U32, name=f"lat_codes{i}", align_bytes=64) for i in range(NT)]
         lat_scales = [one.tile([P, P], U8, name=f"lat_scales{i}", align_bytes=64) for i in range(NT)]
@@ -253,39 +287,46 @@ def tile_multilatentattention_pa_kernel(
         gvs = {}
         gns = {}
 
-        def wb_w(q, ts=(0, 1, 2, 3), engine="s"):
-            if q not in wide:
-                wide[q] = work.tile([P, PACK, GC], BF16, name="wb_wide", bufs=4, align_bytes=64)
-            for t in ts:
-                raw = wb_bytes[q][:, t, :].bitcast(FP8)
-                if engine == "s":
-                    nc.scalar.activation(out=wide[q][:, t, :], in_=raw, func=ACT.Copy, scale=wb_scale[:, t : t + 1])
-                else:
-                    nc.vector.tensor_scalar(
-                        out=wide[q][:, t, :], in0=raw, scalar1=wb_scale[:, t : t + 1], scalar2=None, op0=ALU.mult
-                    )
+        def wb_w(h, t):
+            if h not in wide:
+                wide[h] = work.tile([P, PACK // 2, 2 * GC, 2], BF16, name="wb_wide", align_bytes=64)
+            raw = wb_bytes[t][:, 2 * h * GC : 2 * (h + 1) * GC].bitcast(FP8)
+            nc.vector.tensor_scalar(
+                out=wide[h][:, t // 2, :, t % 2], in0=raw, scalar1=wb_scale[:, t : t + 1], scalar2=None, op0=ALU.mult
+            )
 
-        def wb_iv(q):
-            heads = wide[q][:].rearrange("p t (h c) -> p h c t", h=GH)
-            gvs[q] = work.tile([P, GH, VD, PACK], BF16, name="wb_gv", align_bytes=64)
-            nc.vector.tensor_copy(out=gvs[q][:], in_=heads[:, :, NOPE:, :])
+        def wide_words(h):
+            words = wide[h][:].rearrange("p u n e -> p u (n e)").bitcast(F32)
+            return words.rearrange("p u (h c) -> p h c u", h=2 * GH)
 
-        def wb_in(q):
-            heads = wide[q][:].rearrange("p t (h c) -> p h c t", h=GH)
-            gns[q] = work.tile([P, GH, NOPE, PACK], BF16, name="wb_gn", align_bytes=64)
-            nc.vector.tensor_copy(out=gns[q][:], in_=heads[:, :, :NOPE, :])
+        def word_view(grouped):
+            words = grouped.rearrange("p h c t -> p h (c t)").bitcast(F32)
+            return words.rearrange("p h (c u) -> p h c u", u=2)
+
+        def wb_iv(q, part, engine):
+            if q not in gvs:
+                gvs[q] = work.tile([P, GH, VD, PACK], BF16, name="wb_gv", align_bytes=64)
+            first = (q % 2) * GH + part * GH // 2
+            empty(
+                word_view(gvs[q][:, part * GH // 2 : (part + 1) * GH // 2]),
+                wide_words(q // 2)[:, first : first + GH // 2, NOPE:],
+                engine,
+            )
+
+        def wb_in(h, part, engine):
+            if h not in gns:
+                gns[h] = work.tile([P, 2 * GH, NOPE, PACK], BF16, name="wb_gn", align_bytes=64)
+            some = slice(part * GH, (part + 1) * GH)
+            empty(word_view(gns[h][:, some]), wide_words(h)[:, some, :NOPE], engine)
 
         def wb_qv(q):
             nc.vector.quantize_mx(
                 out=v_codes[q][:].bitcast(FP8X4), scales=v_scales[q][:], in_=gvs[q][:].rearrange("p h c t -> p (h c t)")
             )
 
-        def wb_qn(q):
-            cols = slice((q % 2) * GN, (q % 2 + 1) * GN)
+        def wb_qn(h):
             nc.vector.quantize_mx(
-                out=n_codes[q // 2][:, cols].bitcast(FP8X4),
-                scales=n_scales[q // 2][:, cols],
-                in_=gns[q][:].rearrange("p h c t -> p (h c t)"),
+                out=n_codes[h][:].bitcast(FP8X4), scales=n_scales[h][:], in_=gns[h][:].rearrange("p h c t -> p (h c t)")
             )
 
         banks = {}
@@ -309,203 +350,230 @@ def tile_multilatentattention_pa_kernel(
         def mk(i, h):
             mm2(("k", i, h), i, n_codes[h], n_scales[h])
 
+        v_out = {}
+
         def ov(i, q, engine):
-            v_sb = work.tile([P, GV], F32, name="v_sb", bufs=8)
-            empty(v_sb[:], banks["v", i, q][:], engine)
-            nc.sync.dma_start(out=v_v[i][:, q * GV : (q + 1) * GV], in_=v_sb[:])
+            if (i, q // 2) not in v_out:
+                v_sb = work.tile([P, 2 * GV], F32, name="v_sb", bufs=4)
+                v_out[i, q // 2] = v_sb
+            half = slice((q % 2) * GV, (q % 2 + 1) * GV)
+            empty(v_out[i, q // 2][:, half], banks["v", i, q][:], engine)
+
+        def sv(i, h):
+            nc.sync.dma_start(out=v_v[i][:, 2 * h * GV : 2 * (h + 1) * GV], in_=v_out[i, h][:])
 
         def ok(i, h, engine):
-            empty(k_sb[i][:, :, :NOPE], banks["k", i, h][:].rearrange("p (h c) -> p h c", c=NOPE), engine)
-            nc.sync.dma_start(out=k_v[i][:, 2 * GH * h : 2 * GH * (h + 1), :], in_=k_sb[i][:])
+            empty(k_sb[i, h][:, :, :NOPE], banks["k", i, h][:].rearrange("p (h c) -> p h c", c=NOPE), engine)
+
+        def sk(i, h):
+            nc.sync.dma_start(out=k_v[i][:, 2 * GH * h : 2 * GH * (h + 1), :], in_=k_sb[i, h][:])
 
         with tc.manual_schedule():
-            load_wb(0)
-            wb_w(0, (0,), "s")
-            wb_w(0, (2,), "v")
-            wb_w(0, (1,), "v")
-            load_wb(1)
             load_gb()
-            wb_w(1, (1,), "s")
-            load_wa(2)
-            wb_w(1, (3,), "s")
-            wa_i(2, 480, 640, "s")
-            spread(1, "s")
-            wb_w(1, (2,), "v")
-            wb_w(0, (3,), "v")
-            load_wa(1)
-            load_wa(0, 320, KV)
-            wb_w(1, (0,), "v")
-            wb_in(0)
-            wa_i(2, 320, 480, "v")
-            load_hid(2)
-            wb_iv(0)
-            load_hid(3)
-            hid_t(2, 0)
-            wa_i(1, 480, 640, "v")
-            wb_iv(1)
-            load_wa(0, 0, 320)
-            wa_i(1, 320, 480, "s")
-            wa_i(1, 160, 320, "v")
-            load_hid(0)
-            wb_in(1)
-            wa_i(0, 0, 160, "v")
-            load_wa(3)
-            hid_t(2, 1)
-            wa_i(0, 320, 480, "s")
-            wa_i(2, 0, 160, "s")
-            wa_i(0, 480, 640, "s")
-            wa_i(1, 0, 160, "s")
-            hid_t(3, 0)
-            load_wb(3)
-            hid_c(3, 0, "s")
-            wa_q(1)
-            hid_t(3, 1)
-            load_rot()
-            wa_i(0, 160, 320, "v")
-            hid_c(3, 1, "s")
-            signed_sin()
-            hid_q(3)
-            hid_c(2, 0, "s")
-            wa_i(2, 160, 320, "v")
             load_wb(2)
-            hid_t(0, 0)
-            hid_t(0, 1)
-            hid_c(0, 0, "s")
-            wa_i(3, 320, 480, "s")
+            spread_m()
+            spread_c("s")
+            load_wa(1)
+            wa_m(1, 1)
+            load_wb(1)
+            wa_e(1, 1, "s")
+            wb_w(0, 2)
+            wa_m(1, 0)
+            load_wb(0, 0, 2)
+            wa_e(1, 0, "s")
+            load_wa(0)
+            wa_i(0, 512, 640, "s")
+            load_hid(3)
+            load_wa(3)
+            wa_m(0, 0)
+            wb_w(1, 2)
+            wa_m(0, 1)
+            load_wb(3)
+            wb_w(1, 1)
+            wb_w(0, 1)
+            wa_i(1, 512, 640, "s")
+            wa_e(0, 0, "s")
+            load_wa(2)
+            wa_e(0, 1, "s")
+            wa_q(1)
+            load_hid(0)
+            hid_t(3, 1)
+            hid_t(3, 0)
+            wb_w(0, 0)
+            wa_i(3, 256, 512, "s")
+            hid_c(3, 1, "s")
+            load_wb(0, 2, 4)
             wa_q(0)
-            mm1(3, 0)
-            mm1(3, 1)
-            wa_i(3, 480, 640, "s")
-            wa_i(3, 0, 160, "v")
-            wb_qn(1)
-            wa_q(2)
+            wb_w(0, 3)
+            wa_m(3, 0)
+            load_rot()
+            wa_m(2, 0)
+            signed_sin()
+            wa_i(3, 512, 640, "s")
             load_hid(1)
-            wa_i(3, 160, 320, "s")
+            hid_t(0, 1)
+            wb_w(1, 3)
+            hid_c(3, 0, "s")
+            wb_iv(0, 0, "v")
+            hid_q(3)
+            wa_i(2, 512, 640, "s")
+            wb_w(1, 0)
+            wb_iv(0, 1, "s")
+            wa_m(2, 1)
+            wa_e(3, 0, "s")
+            load_hid(2)
+            mm1(3, 0)
             wa_q(3)
-            hid_c(2, 1, "s")
-            hid_q(2)
-            hid_c(0, 1, "s")
-            spread(0, "s")
-            mm1(3, 2)
-            mm1(3, 3)
-            wb_w(3, (2,), "s")
-            wb_w(2, (3,), "s")
-            wb_w(2, (0,), "s")
-            hid_q(0)
-            bn(3)
-            rope_a(3)
-            cen(3)
-            mm1(2, 0)
-            mm1(2, 1)
-            mm1(2, 2)
-            mm1(2, 3)
-            wb_qn(0)
-            wb_w(3, (3,), "s")
-            fin(3)
-            mm1(0, 0)
-            wb_qv(1)
-            hid_t(1, 0)
-            lat_t(3)
-            bn(2)
-            wb_w(3, (0,), "s")
-            lat_c(3, "s")
-            mm1(0, 1)
-            mm1(0, 2)
-            lat_q(3)
-            rope_b(3)
-            wb_w(3, (1,), "s")
-            hid_c(1, 0, "s")
-            mv(3, 1)
-            ov(3, 1, "s")
-            mk(3, 0)
-            cen(2)
-            rope_r(3)
-            fin(2)
+            wa_e(2, 0, "s")
+            wa_e(2, 1, "s")
+            wa_q(2)
             hid_t(1, 1)
-            ok(3, 0, "s")
-            lat_t(2)
+            hid_t(1, 0)
             hid_c(1, 1, "s")
+            mm1(3, 1)
+            mm1(3, 2)
+            hid_c(1, 0, "s")
+            mm1(3, 3)
+            wb_in(0, 0, "s")
+            wb_in(1, 0, "s")
             wb_qv(0)
-            lat_c(2, "s")
-            rope_a(2)
-            wb_in(3)
-            mv(3, 0)
-            lat_q(2)
-            rope_b(2)
-            wb_w(2, (2,), "s")
-            mm1(0, 3)
-            ov(3, 0, "s")
-            mk(2, 0)
+            hid_t(0, 0)
             hid_q(1)
-            wb_w(2, (1,), "s")
-            rope_r(2)
-            bn(0)
-            ok(2, 0, "s")
-            wb_in(2)
-            wb_qn(3)
-            mv(2, 1)
-            wb_qn(2)
-            cen(0)
             mm1(1, 0)
             mm1(1, 1)
+            hid_c(0, 1, "s")
+            bn_s(3)
+            wb_iv(1, 0, "v")
+            hid_c(0, 0, "s")
+            wb_in(1, 1, "s")
+            bn_a(3)
+            wb_iv(3, 0, "s")
             mm1(1, 2)
-            fin(0)
-            mv(2, 0)
+            rope_a(3)
+            cen(3)
+            hid_q(0)
+            wb_in(0, 1, "s")
+            fin(3)
             mm1(1, 3)
-            ov(2, 1, "s")
-            ov(2, 0, "s")
+            wb_qn(1)
+            bn_s(1)
+            wb_qn(0)
+            wb_iv(1, 1, "s")
+            hid_t(2, 0)
+            lat_t(3)
+            mm1(0, 0)
+            lat_c(3, "s")
+            lat_q(3)
+            rope_b(3)
+            rope_r(3, 0, "s")
+            hid_c(2, 0, "s")
+            mm1(0, 1)
+            mk(3, 0)
+            bn_a(1)
             mk(3, 1)
+            ok(3, 0, "s")
+            mv(3, 0)
+            wb_qv(1)
+            sk(3, 0)
             ok(3, 1, "s")
-            mk(2, 1)
-            ok(2, 1, "s")
-            lat_t(0)
-            bn(1)
-            lat_c(0, "s")
-            rope_a(0)
-            lat_q(0)
-            mv(0, 0)
             cen(1)
-            mk(0, 0)
-            rope_b(0)
-            fin(1)
-            lat_t(1)
-            ov(0, 0, "s")
-            rope_r(0)
-            ok(0, 0, "s")
             rope_a(1)
+            rope_b(1)
+            mv(3, 1)
+            ov(3, 0, "s")
+            ov(3, 1, "s")
+            fin(1)
+            rope_r(3, 1, "v")
+            wb_iv(2, 0, "v")
+            wb_iv(3, 1, "v")
+            wb_iv(2, 1, "v")
+            hid_t(2, 1)
+            lat_t(1)
             lat_c(1, "s")
             lat_q(1)
-            rope_b(1)
-            rope_r(1)
-            mv(0, 1)
-            mk(1, 0)
-            wb_iv(3)
-            ov(0, 1, "s")
-            mv(1, 1)
-            mk(1, 1)
-            wb_iv(2)
-            ok(1, 0, "s")
-            mk(0, 1)
-            ok(0, 1, "s")
-            ov(1, 1, "s")
-            wb_qv(2)
+            hid_c(2, 1, "s")
+            mm1(0, 2)
+            sk(3, 1)
+            mm1(0, 3)
+            rope_r(1, 0, "s")
+            sv(3, 0)
             wb_qv(3)
+            mk(1, 0)
+            mv(1, 1)
+            wb_qv(2)
+            ok(1, 0, "s")
+            bn_s(0)
             mv(1, 0)
-            mv(1, 2)
-            mv(3, 3)
-            mv(2, 3)
-            ok(1, 1, "s")
-            mv(2, 2)
-            mv(0, 2)
-            ov(1, 2, "s")
-            mv(0, 3)
-            ov(1, 0, "s")
-            ov(2, 2, "v")
-            mv(1, 3)
-            ov(0, 2, "s")
-            ov(2, 3, "v")
+            sk(1, 0)
+            ov(1, 1, "s")
+            hid_q(2)
             mv(3, 2)
+            ov(1, 0, "s")
             ov(3, 2, "s")
-            ov(1, 3, "s")
+            mv(3, 3)
+            mv(1, 2)
+            bn_a(0)
+            sv(1, 0)
             ov(3, 3, "v")
+            ov(1, 2, "s")
+            sv(3, 1)
+            cen(0)
+            mm1(2, 0)
+            fin(0)
+            mm1(2, 1)
+            mv(1, 3)
+            mm1(2, 2)
+            rope_a(0)
+            rope_b(0)
+            ov(1, 3, "s")
+            sv(1, 1)
+            mm1(2, 3)
+            lat_t(0)
+            mk(1, 1)
+            lat_c(0, "s")
+            bn_s(2)
+            bn_a(2)
+            lat_q(0)
+            ok(1, 1, "s")
+            mk(0, 0)
+            ok(0, 0, "s")
+            mv(0, 1)
+            cen(2)
+            sk(1, 1)
+            rope_r(0, 0, "v")
+            mv(0, 0)
+            fin(2)
+            ov(0, 0, "v")
+            ov(0, 1, "s")
+            mv(0, 3)
+            sk(0, 0)
+            mv(0, 2)
             ov(0, 3, "s")
+            ov(0, 2, "v")
+            lat_t(2)
+            mk(0, 1)
+            rope_a(2)
+            lat_c(2, "s")
+            lat_q(2)
+            mk(2, 0)
+            mv(2, 0)
+            ok(2, 0, "s")
+            ov(2, 0, "s")
+            mv(2, 1)
+            rope_b(2)
+            rope_r(2, 0, "v")
+            sv(0, 0)
+            mv(2, 3)
+            sv(0, 1)
+            sk(2, 0)
+            ov(2, 1, "v")
+            mv(2, 2)
+            mk(2, 1)
+            ok(0, 1, "v")
+            ov(2, 2, "s")
+            sv(2, 0)
+            sk(0, 1)
+            ov(2, 3, "s")
+            ok(2, 1, "s")
+            sv(2, 1)
+            sk(2, 1)

@@ -3,6 +3,7 @@ from contextlib import ExitStack
 import concourse.mybir as mybir
 from concourse.masks import make_identity
 
+DIRECT = 1
 T, HID, H, NOPE, ROPE, VD, LAT = 512, 2048, 16, 64, 128, 128, 512
 HALF = ROPE // 2
 KV = LAT + ROPE
@@ -29,7 +30,6 @@ NHG = H // GH
 GC = GH * HEAD
 GV = GH * VD
 GN = GH * NOPE
-S_COL = 480
 
 
 def tile_multilatentattention_pa_kernel(
@@ -138,9 +138,9 @@ def tile_multilatentattention_pa_kernel(
             for m in range(2):
                 c0 = 256 * j + P * m
                 nc.tensor.matmul(
-                    bank[:, P * m : P * (m + 1), :],
+                    bank[:, P * m : P * (m + 1), :].rearrange("p c t -> p t c"),
                     lhsT=ident_bf[:],
-                    rhs=wa_raw[g][:, :, c0 : c0 + P].rearrange("p t c -> p c t"),
+                    rhs=wa_raw[g][:, :, c0 : c0 + P],
                     start=True,
                     stop=True,
                 )
@@ -150,12 +150,11 @@ def tile_multilatentattention_pa_kernel(
             out = wa_grouped[g][:, 256 * j : 256 * (j + 1), :].rearrange("p c t -> p (c t)")
             empty(out, wa_bank[g, j][:].rearrange("p c t -> p (c t)"), engine)
 
-        def wa_q(g):
+        def wa_q(g, a, b):
             flat = wa_grouped[g][:].rearrange("p c t -> p (c t)")
-            for a, b in ((0, LAT), (LAT, KV)):
-                nc.vector.quantize_mx(
-                    out=wa_codes[g][:, a:b].bitcast(FP8X4), scales=wa_scales[g][:, a:b], in_=flat[:, a * PACK : b * PACK]
-                )
+            nc.vector.quantize_mx(
+                out=wa_codes[g][:, a:b].bitcast(FP8X4), scales=wa_scales[g][:, a:b], in_=flat[:, a * PACK : b * PACK]
+            )
 
         hid_grouped = [one.tile([P, NG * P * PACK], BF16, name=f"hid_grouped{i}", align_bytes=64) for i in range(NT)]
 
@@ -180,25 +179,34 @@ def tile_multilatentattention_pa_kernel(
         kv = {}
         rp = {}
 
-        def mm1(i, g):
-            if g == 0:
-                kv[i] = psum.tile([P, LAT], F32, name="bank", tag="bank")
-                rp[i] = psum.tile([P, 512], F32, name="bank", tag="bank")
+        def mm1(dst, i, g, a, b):
             toks = slice(g * P, (g + 1) * P)
-            for dst, a, b in ((kv[i][:], 0, LAT), (rp[i][:, 0:ROPE], LAT, KV)):
-                nc.tensor.matmul_mx(
-                    out=dst,
-                    lhsT=hid_codes[i][:, toks].bitcast(FP8X4),
-                    lhsT_scale=hid_scales[i][:, toks],
-                    rhs=wa_codes[g][:, a:b].bitcast(FP8X4),
-                    rhs_scale=wa_scales[g][:, a:b],
-                    start=(g == 0),
-                    stop=(g == NG - 1),
-                )
+            nc.tensor.matmul_mx(
+                out=dst,
+                lhsT=hid_codes[i][:, toks].bitcast(FP8X4),
+                lhsT_scale=hid_scales[i][:, toks],
+                rhs=wa_codes[g][:, a:b].bitcast(FP8X4),
+                rhs_scale=wa_scales[g][:, a:b],
+                start=(g == 0),
+                stop=(g == NG - 1),
+            )
+
+        def mml(i, g):
+            if g == 0:
+                bank = psum.tile([P, LAT], F32, name="bank", tag="bank")
+                kv[i] = bank
+            mm1(kv[i][:], i, g, 0, LAT)
+
+        def mmr(i, g):
+            if g == 0:
+                bank = psum.tile([P, 512], F32, name="bank", tag="bank")
+                rp[i] = bank
+            mm1(rp[i][:, 0:ROPE], i, g, LAT, KV)
 
         lat = {}
-        k_sb = {(i, 0): one.tile([P, 2 * GH, NOPE + ROPE], F32, name=f"k_sb{i}", align_bytes=64) for i in range(NT)}
-        for i in range(NT - 1):
+        k_sb = {}
+        for i in range(DIRECT, NT):
+            k_sb[i, 0] = one.tile([P, 2 * GH, NOPE + ROPE], F32, name=f"k_sb{i}", align_bytes=64)
             k_sb[i, 1] = k_sb[i, 0]
         k_sb[NT - 1, 1] = one.tile([P, 2 * GH, NOPE + ROPE], F32, name="k_sb_last", align_bytes=64)
 
@@ -249,13 +257,17 @@ def tile_multilatentattention_pa_kernel(
         def rope_b(i):
             xc, xs = rots[i]
             r = work.tile([P, ROPE], F32, name="r", bufs=4)
-            nc.gpsimd.tensor_tensor(
+            nc.vector.tensor_tensor(
                 out=r[:].rearrange("p (c two) -> p c two", two=2), in0=xc[:], in1=xs[:], op=ALU.add
             )
             rots[i] = r
 
-        def rope_r(i, h, engine):
-            empty(k_sb[i, h][:, :, NOPE:], rots[i][:].unsqueeze(1).to_broadcast([P, 2 * GH, ROPE]), engine)
+        def rope_d(i):
+            nc.sync.dma_start(out=k_v[i][:, :, NOPE:], in_=rots[i][:].unsqueeze(1).to_broadcast([P, H, ROPE]))
+
+        def rope_r(i, h, a, b, engine):
+            copies = rots[i][:].unsqueeze(1).to_broadcast([P, (b - a) * GH, ROPE])
+            empty(k_sb[i, h][:, a * GH : b * GH, NOPE:], copies, engine)
 
         lat_codes = [one.tile([P, P], U32, name=f"lat_codes{i}", align_bytes=64) for i in range(NT)]
         lat_scales = [one.tile([P, P], U8, name=f"lat_scales{i}", align_bytes=64) for i in range(NT)]
@@ -287,12 +299,12 @@ def tile_multilatentattention_pa_kernel(
         gvs = {}
         gns = {}
 
-        def wb_w(h, t):
+        def wb_w(h, t, a, b):
             if h not in wide:
                 wide[h] = work.tile([P, PACK // 2, 2 * GC, 2], BF16, name="wb_wide", align_bytes=64)
-            raw = wb_bytes[t][:, 2 * h * GC : 2 * (h + 1) * GC].bitcast(FP8)
+            raw = wb_bytes[t][:, (2 * h + a) * GC : (2 * h + b) * GC].bitcast(FP8)
             nc.vector.tensor_scalar(
-                out=wide[h][:, t // 2, :, t % 2], in0=raw, scalar1=wb_scale[:, t : t + 1], scalar2=None, op0=ALU.mult
+                out=wide[h][:, t // 2, a * GC : b * GC, t % 2], in0=raw, scalar1=wb_scale[:, t : t + 1], scalar2=None, op0=ALU.mult
             )
 
         def wide_words(h):
@@ -324,31 +336,34 @@ def tile_multilatentattention_pa_kernel(
                 out=v_codes[q][:].bitcast(FP8X4), scales=v_scales[q][:], in_=gvs[q][:].rearrange("p h c t -> p (h c t)")
             )
 
-        def wb_qn(h):
+        def wb_qn(h, a, b):
             nc.vector.quantize_mx(
-                out=n_codes[h][:].bitcast(FP8X4), scales=n_scales[h][:], in_=gns[h][:].rearrange("p h c t -> p (h c t)")
+                out=n_codes[h][:, a * GN : b * GN].bitcast(FP8X4),
+                scales=n_scales[h][:, a * GN : b * GN],
+                in_=gns[h][:, a * GH : b * GH].rearrange("p h c t -> p (h c t)"),
             )
 
         banks = {}
 
-        def mm2(key, i, codes, scales):
+        def mm2(key, i, codes, scales, n=512):
             bank = psum.tile([P, 512], F32, name="bank", tag="bank")
             nc.tensor.matmul_mx(
-                out=bank[:],
+                out=bank[:, 0:n],
                 lhsT=lat_codes[i][:].bitcast(FP8X4),
                 lhsT_scale=lat_scales[i][:],
-                rhs=codes[:].bitcast(FP8X4),
-                rhs_scale=scales[:],
+                rhs=codes.bitcast(FP8X4),
+                rhs_scale=scales,
                 start=True,
                 stop=True,
             )
             banks[key] = bank
 
         def mv(i, q):
-            mm2(("v", i, q), i, v_codes[q], v_scales[q])
+            mm2(("v", i, q), i, v_codes[q][:], v_scales[q][:])
 
-        def mk(i, h):
-            mm2(("k", i, h), i, n_codes[h], n_scales[h])
+        def mk(i, h, a, b):
+            cols = slice(a * GN, b * GN)
+            mm2(("k", i, h, a), i, n_codes[h][:, cols], n_scales[h][:, cols], (b - a) * GN)
 
         v_out = {}
 
@@ -359,221 +374,256 @@ def tile_multilatentattention_pa_kernel(
             half = slice((q % 2) * GV, (q % 2 + 1) * GV)
             empty(v_out[i, q // 2][:, half], banks["v", i, q][:], engine)
 
-        def sv(i, h):
-            nc.sync.dma_start(out=v_v[i][:, 2 * h * GV : 2 * (h + 1) * GV], in_=v_out[i, h][:])
+        def sv(i, h, a, b):
+            nc.sync.dma_start(out=v_v[i][:, (2 * h + a) * GV : (2 * h + b) * GV], in_=v_out[i, h][:, a * GV : b * GV])
 
-        def ok(i, h, engine):
-            empty(k_sb[i, h][:, :, :NOPE], banks["k", i, h][:].rearrange("p (h c) -> p h c", c=NOPE), engine)
+        n_out = {}
 
-        def sk(i, h):
-            nc.sync.dma_start(out=k_v[i][:, 2 * GH * h : 2 * GH * (h + 1), :], in_=k_sb[i, h][:])
+        def ok(i, h, a, b, engine):
+            keys = banks["k", i, h, a][:, 0 : (b - a) * GN].rearrange("p (h c) -> p h c", c=NOPE)
+            if i < DIRECT:
+                n_sb = work.tile([P, 2 * GH, NOPE], F32, name="n_sb", bufs=3)
+                n_out[i, h] = n_sb
+                empty(n_sb[:], keys, engine)
+            else:
+                empty(k_sb[i, h][:, a * GH : b * GH, :NOPE], keys, engine)
+
+        def sk(i, h, a, b):
+            heads = slice((2 * h + a) * GH, (2 * h + b) * GH)
+            if i < DIRECT:
+                nc.sync.dma_start(out=k_v[i][:, heads, :NOPE], in_=n_out[i, h][:])
+            else:
+                nc.sync.dma_start(out=k_v[i][:, heads, :], in_=k_sb[i, h][:, a * GH : b * GH, :])
 
         with tc.manual_schedule():
+            load_wb(0, 2, 4)
+            load_wb(2, 0, 2)
             load_gb()
-            load_wb(2)
+            load_wa(1)
+            wa_i(1, 512, 640, "s")
+            load_wb(1, 2, 4)
+            wb_w(1, 0, 0, 2)
+            wb_w(0, 2, 0, 2)
             spread_m()
             spread_c("s")
-            load_wa(1)
             wa_m(1, 1)
-            load_wb(1)
-            wa_e(1, 1, "s")
-            wb_w(0, 2)
+            load_wb(2, 2, 4)
+            wb_w(1, 1, 0, 2)
+            wb_w(1, 2, 0, 2)
+            load_wb(3, 2, 4)
+            load_wa(2)
             wa_m(1, 0)
-            load_wb(0, 0, 2)
-            wa_e(1, 0, "s")
+            wa_m(2, 0)
+            wa_e(1, 1, "s")
+            wa_m(2, 1)
+            wa_i(2, 512, 640, "s")
             load_wa(0)
-            wa_i(0, 512, 640, "s")
+            load_wb(0, 0, 2)
             load_hid(3)
+            wa_e(1, 0, "s")
+            wb_w(1, 3, 0, 2)
+            wa_q(1, 0, 512)
+            wb_in(1, 1, "v")
+            wa_i(0, 512, 640, "s")
+            load_wb(3, 0, 2)
+            hid_t(3, 1)
+            wb_w(0, 0, 0, 2)
+            wb_w(0, 3, 0, 2)
+            wb_iv(3, 0, "s")
+            wb_iv(3, 1, "s")
+            wa_e(2, 0, "s")
+            load_rot()
+            wa_e(2, 1, "s")
+            wa_m(0, 1)
+            wb_in(1, 0, "s")
+            hid_c(3, 1, "s")
             load_wa(3)
             wa_m(0, 0)
-            wb_w(1, 2)
-            wa_m(0, 1)
-            load_wb(3)
-            wb_w(1, 1)
-            wb_w(0, 1)
-            wa_i(1, 512, 640, "s")
-            wa_e(0, 0, "s")
-            load_wa(2)
-            wa_e(0, 1, "s")
-            wa_q(1)
-            load_hid(0)
-            hid_t(3, 1)
-            hid_t(3, 0)
-            wb_w(0, 0)
-            wa_i(3, 256, 512, "s")
-            hid_c(3, 1, "s")
-            load_wb(0, 2, 4)
-            wa_q(0)
-            wb_w(0, 3)
-            wa_m(3, 0)
-            load_rot()
-            wa_m(2, 0)
-            signed_sin()
-            wa_i(3, 512, 640, "s")
-            load_hid(1)
-            hid_t(0, 1)
-            wb_w(1, 3)
-            hid_c(3, 0, "s")
-            wb_iv(0, 0, "v")
-            hid_q(3)
-            wa_i(2, 512, 640, "s")
-            wb_w(1, 0)
-            wb_iv(0, 1, "s")
-            wa_m(2, 1)
-            wa_e(3, 0, "s")
-            load_hid(2)
-            mm1(3, 0)
-            wa_q(3)
-            wa_e(2, 0, "s")
-            wa_e(2, 1, "s")
-            wa_q(2)
-            hid_t(1, 1)
-            hid_t(1, 0)
-            hid_c(1, 1, "s")
-            mm1(3, 1)
-            mm1(3, 2)
-            hid_c(1, 0, "s")
-            mm1(3, 3)
-            wb_in(0, 0, "s")
-            wb_in(1, 0, "s")
-            wb_qv(0)
-            hid_t(0, 0)
-            hid_q(1)
-            mm1(1, 0)
-            mm1(1, 1)
-            hid_c(0, 1, "s")
-            bn_s(3)
-            wb_iv(1, 0, "v")
-            hid_c(0, 0, "s")
-            wb_in(1, 1, "s")
-            bn_a(3)
-            wb_iv(3, 0, "s")
-            mm1(1, 2)
-            rope_a(3)
-            cen(3)
-            hid_q(0)
-            wb_in(0, 1, "s")
-            fin(3)
-            mm1(1, 3)
-            wb_qn(1)
-            bn_s(1)
-            wb_qn(0)
-            wb_iv(1, 1, "s")
-            hid_t(2, 0)
-            lat_t(3)
-            mm1(0, 0)
-            lat_c(3, "s")
-            lat_q(3)
-            rope_b(3)
-            rope_r(3, 0, "s")
-            hid_c(2, 0, "s")
-            mm1(0, 1)
-            mk(3, 0)
-            bn_a(1)
-            mk(3, 1)
-            ok(3, 0, "s")
-            mv(3, 0)
-            wb_qv(1)
-            sk(3, 0)
-            ok(3, 1, "s")
-            cen(1)
-            rope_a(1)
-            rope_b(1)
-            mv(3, 1)
-            ov(3, 0, "s")
-            ov(3, 1, "s")
-            fin(1)
-            rope_r(3, 1, "v")
-            wb_iv(2, 0, "v")
-            wb_iv(3, 1, "v")
-            wb_iv(2, 1, "v")
-            hid_t(2, 1)
-            lat_t(1)
-            lat_c(1, "s")
-            lat_q(1)
-            hid_c(2, 1, "s")
-            mm1(0, 2)
-            sk(3, 1)
-            mm1(0, 3)
-            rope_r(1, 0, "s")
-            sv(3, 0)
             wb_qv(3)
-            mk(1, 0)
-            mv(1, 1)
-            wb_qv(2)
-            ok(1, 0, "s")
-            bn_s(0)
-            mv(1, 0)
-            sk(1, 0)
-            ov(1, 1, "s")
-            hid_q(2)
-            mv(3, 2)
-            ov(1, 0, "s")
-            ov(3, 2, "s")
-            mv(3, 3)
-            mv(1, 2)
-            bn_a(0)
-            sv(1, 0)
-            ov(3, 3, "v")
-            ov(1, 2, "s")
-            sv(3, 1)
-            cen(0)
-            mm1(2, 0)
-            fin(0)
-            mm1(2, 1)
-            mv(1, 3)
-            mm1(2, 2)
+            wa_q(1, 512, 640)
+            wa_q(2, 512, 640)
+            wa_e(0, 1, "s")
+            hid_t(3, 0)
+            wa_q(2, 0, 512)
+            load_wb(1, 0, 2)
+            wa_i(3, 512, 640, "v")
+            wa_q(0, 512, 640)
+            wb_w(0, 1, 0, 2)
+            wa_i(3, 256, 512, "s")
+            signed_sin()
+            wa_q(3, 512, 640)
+            load_hid(2)
+            wa_m(3, 0)
+            hid_c(3, 0, "s")
+            hid_q(3)
+            load_hid(0)
+            wa_e(0, 0, "s")
+            wa_e(3, 0, "s")
+            hid_t(0, 0)
+            hid_t(0, 1)
+            wa_q(0, 0, 512)
+            mmr(3, 0)
+            mml(3, 0)
+            mml(3, 1)
+            mml(3, 2)
+            wb_qn(1, 0, 2)
+            hid_c(0, 0, "s")
+            mmr(3, 1)
+            wa_q(3, 0, 512)
+            hid_c(0, 1, "s")
+            hid_q(0)
+            load_hid(1)
+            mmr(3, 2)
+            mmr(3, 3)
+            mml(3, 3)
+            mmr(0, 0)
+            rope_a(3)
+            wb_iv(0, 0, "s")
+            wb_iv(2, 0, "s")
+            mmr(0, 1)
+            mmr(0, 2)
+            mmr(0, 3)
+            wb_iv(2, 1, "s")
+            bn_s(3)
+            rope_b(3)
+            hid_t(1, 0)
+            bn_a(3)
             rope_a(0)
+            wb_in(0, 0, "s")
+            cen(3)
+            hid_c(1, 0, "s")
+            hid_t(1, 1)
+            mml(0, 0)
+            hid_c(1, 1, "s")
+            mml(0, 1)
+            mml(0, 2)
             rope_b(0)
-            ov(1, 3, "s")
-            sv(1, 1)
-            mm1(2, 3)
+            fin(3)
+            hid_q(1)
+            mml(0, 3)
+            bn_s(0)
+            lat_t(3)
+            rope_r(3, 0, 0, 2, "s")
+            lat_c(3, "s")
+            hid_t(2, 0)
+            wb_in(0, 1, "v")
+            rope_d(0)
+            bn_a(0)
+            mml(1, 0)
+            mml(1, 1)
+            rope_r(3, 1, 0, 2, "s")
+            lat_q(3)
+            mk(3, 1, 0, 2)
+            ok(3, 1, 0, 2, "s")
+            cen(0)
+            wb_qn(0, 0, 2)
+            mml(1, 2)
+            mml(1, 3)
+            hid_c(2, 0, "s")
+            mk(3, 0, 0, 2)
+            mmr(1, 0)
+            fin(0)
+            mmr(1, 1)
+            mmr(1, 2)
             lat_t(0)
-            mk(1, 1)
-            lat_c(0, "s")
-            bn_s(2)
-            bn_a(2)
+            ok(3, 0, 0, 2, "s")
+            sk(3, 1, 0, 2)
+            mv(3, 3)
+            wb_iv(0, 1, "s")
+            mmr(1, 3)
+            wb_qv(2)
+            mv(3, 2)
+            bn_s(1)
+            hid_t(2, 1)
+            ov(3, 3, "s")
+            lat_c(0, "v")
+            bn_a(1)
+            ov(3, 2, "s")
             lat_q(0)
-            ok(1, 1, "s")
-            mk(0, 0)
-            ok(0, 0, "s")
+            hid_c(2, 1, "s")
+            mk(0, 0, 0, 2)
+            ok(0, 0, 0, 2, "s")
+            mk(0, 1, 0, 2)
+            cen(1)
+            mv(0, 2)
+            rope_a(1)
+            mv(0, 3)
+            fin(1)
+            lat_t(1)
+            hid_q(2)
+            ov(0, 2, "v")
+            mml(2, 0)
+            mml(2, 1)
+            mml(2, 2)
+            rope_b(1)
+            ok(0, 1, 0, 2, "s")
+            sk(3, 0, 0, 2)
+            ov(0, 3, "s")
+            sv(3, 1, 0, 2)
+            wb_qv(0)
+            lat_c(1, "s")
+            wb_iv(1, 0, "s")
+            lat_q(1)
+            mml(2, 3)
+            wb_iv(1, 1, "s")
+            mmr(2, 0)
+            mk(1, 0, 0, 2)
+            sk(0, 0, 0, 2)
+            mv(1, 3)
+            mmr(2, 1)
+            mv(3, 0)
+            rope_r(1, 0, 0, 2, "v")
+            bn_s(2)
+            wb_qv(1)
+            mv(1, 2)
+            ok(1, 0, 0, 2, "s")
+            mv(3, 1)
+            ov(1, 3, "s")
+            mmr(2, 2)
+            ov(1, 2, "s")
+            ov(3, 1, "s")
+            bn_a(2)
+            ov(3, 0, "v")
+            mv(1, 1)
+            ov(1, 1, "s")
             mv(0, 1)
             cen(2)
-            sk(1, 1)
-            rope_r(0, 0, "v")
-            mv(0, 0)
+            mv(1, 0)
             fin(2)
-            ov(0, 0, "v")
-            ov(0, 1, "s")
-            mv(0, 3)
-            sk(0, 0)
-            mv(0, 2)
-            ov(0, 3, "s")
-            ov(0, 2, "v")
-            lat_t(2)
-            mk(0, 1)
+            mk(1, 1, 0, 2)
+            sk(0, 1, 0, 2)
+            mmr(2, 3)
+            ov(1, 0, "s")
+            sv(0, 1, 0, 2)
             rope_a(2)
-            lat_c(2, "s")
-            lat_q(2)
-            mk(2, 0)
-            mv(2, 0)
-            ok(2, 0, "s")
-            ov(2, 0, "s")
-            mv(2, 1)
+            lat_t(2)
+            lat_c(2, "v")
             rope_b(2)
-            rope_r(2, 0, "v")
-            sv(0, 0)
-            mv(2, 3)
-            sv(0, 1)
-            sk(2, 0)
+            mv(0, 0)
+            lat_q(2)
+            mk(2, 0, 0, 2)
+            sk(1, 0, 0, 2)
+            ok(1, 1, 0, 2, "s")
+            mv(2, 0)
+            ov(0, 0, "v")
+            sv(1, 1, 0, 2)
+            rope_r(2, 0, 0, 2, "v")
+            sv(3, 0, 0, 2)
+            ov(0, 1, "s")
+            mv(2, 1)
             ov(2, 1, "v")
             mv(2, 2)
-            mk(2, 1)
-            ok(0, 1, "v")
+            sv(1, 0, 0, 2)
+            ok(2, 0, 0, 2, "s")
+            ov(2, 0, "s")
+            sk(1, 1, 0, 2)
+            mv(2, 3)
+            sk(2, 0, 0, 2)
             ov(2, 2, "s")
-            sv(2, 0)
-            sk(0, 1)
-            ov(2, 3, "s")
-            ok(2, 1, "s")
-            sv(2, 1)
-            sk(2, 1)
+            mk(2, 1, 0, 2)
+            ok(2, 1, 0, 2, "s")
+            ov(2, 3, "v")
+            sv(0, 0, 0, 2)
+            sv(2, 0, 0, 2)
+            sv(2, 1, 0, 2)
+            sk(2, 1, 0, 2)

from contextlib import ExitStack

import concourse.mybir as mybir
from concourse.masks import make_identity

DIRECT = 1
T, HID, H, NOPE, ROPE, VD, LAT = 512, 2048, 16, 64, 128, 128, 512
HALF = ROPE // 2
KV = LAT + ROPE
HEAD = NOPE + VD
EPS = 1e-5

FLOPS = 2 * T * HID * KV + 2 * T * LAT * H * HEAD

F32 = mybir.dt.float32
BF16 = mybir.dt.bfloat16
U32 = mybir.dt.uint32
U8 = mybir.dt.uint8
FP8 = mybir.dt.float8_e4m3fn
FP8X4 = mybir.dt.float8_e4m3fn_x4
ALU = mybir.AluOpType
ACT = mybir.ActivationFunctionType

P = 128
PACK = 4
NG = HID // (P * PACK)
NT = T // P
GH = 4
NHG = H // GH
GC = GH * HEAD
GV = GH * VD
GN = GH * NOPE


def tile_multilatentattention_pa_kernel(
    tc, hidden_states, rope_cos, rope_sin, wkv_a, kv_gamma, kv_beta, wkv_b_bytes, wkv_b_scale, out_k, out_v
):
    nc = tc.nc
    with ExitStack() as ctx:
        one = ctx.enter_context(tc.tile_pool(name="one", bufs=1))
        work = ctx.enter_context(tc.tile_pool(name="work", bufs=2))
        psum = ctx.enter_context(tc.psum_pool(name="psum", bufs=8))

        hid_v = hidden_states.rearrange("b (p i) k -> i p (b k)", i=NT)
        cos_v = rope_cos.rearrange("(p i) c -> p i c", i=NT)
        sin_v = rope_sin.rearrange("(p i) c -> p i c", i=NT)
        wa_v = wkv_a.rearrange("(g p t) w -> g p t w", p=P, t=PACK)
        wb_v = wkv_b_bytes.rearrange("(p t) n -> p t n", t=PACK)
        scale_v = wkv_b_scale.rearrange("(p t) o -> p (t o)", t=PACK)
        k_v = out_k.rearrange("b (p i) h c -> i p (b h) c", i=NT)
        v_v = out_v.rearrange("b (p i) h c -> i p (b h c)", i=NT)

        ident = one.tile([P, P], F32, name="ident", align_bytes=64)
        make_identity(nc, ident[:])
        ident_bf = one.tile([P, P], BF16, name="ident_bf", align_bytes=64)
        make_identity(nc, ident_bf[:])
        neg_half = one.tile([P, 1], F32, name="neg_half")
        nc.gpsimd.memset(neg_half[:], -0.5)
        gb_rows = one.tile([P, 2 * LAT], BF16, name="gb_rows", align_bytes=64)
        nc.vector.memset(gb_rows[:], 0.0)
        ones = one.tile([P, P], BF16, name="ones", align_bytes=64)
        nc.vector.memset(ones[:], 1.0)

        wb_scale = one.tile([P, PACK], F32, name="wb_scale")
        nc.scalar.dma_start(out=wb_scale[:], in_=scale_v)
        wa_raw = [one.tile([P, PACK, KV], BF16, name=f"wa_raw{g}", align_bytes=64) for g in range(NG)]
        hid = [one.tile([P, HID], BF16, name=f"hid{i}", align_bytes=64) for i in range(NT)]
        wb_bytes = [one.tile([P, NHG * GC], U8, name=f"wb_bytes{t}", align_bytes=64) for t in range(PACK)]
        cos = one.tile([P, NT, HALF], BF16, name="cos")
        sin = one.tile([P, NT, HALF], BF16, name="sin")

        def load_wa(g, a=0, b=KV):
            nc.sync.dma_start(out=wa_raw[g][:, :, a:b], in_=wa_v[g][:, :, a:b])

        def load_hid(i):
            nc.sync.dma_start(out=hid[i][:], in_=hid_v[i])

        def load_wb(t, a=0, b=NHG):
            cols = slice(a * GC, b * GC)
            nc.sync.dma_start(out=wb_bytes[t][:, cols], in_=wb_v[:, t, cols])

        def load_gb():
            nc.sync.dma_start(out=gb_rows[0:1, 0:LAT], in_=kv_gamma.rearrange("(o c) -> o c", o=1))
            nc.sync.dma_start(out=gb_rows[0:1, LAT:], in_=kv_beta.rearrange("(o c) -> o c", o=1))

        def load_rot():
            nc.sync.dma_start(out=cos[:], in_=cos_v)
            nc.sync.dma_start(out=sin[:], in_=sin_v)

        def empty(out, in_, engine):
            if engine == "s":
                nc.scalar.copy(out=out, in_=in_)
            else:
                nc.vector.tensor_copy(out=out, in_=in_)

        gamma_beta = one.tile([P, 2 * LAT], BF16, name="gamma_beta", align_bytes=64)
        gamma = gamma_beta[:, 0:LAT]
        beta = gamma_beta[:, LAT:]
        spread_bank = {}

        def spread_m():
            bank = psum.tile([P, 2 * LAT], BF16, name="bank", tag="bank")
            for j in range(2):
                half = slice(j * LAT, (j + 1) * LAT)
                nc.tensor.matmul(bank[:, half], lhsT=ones[:], rhs=gb_rows[:, half], start=True, stop=True)
            spread_bank[0] = bank

        def spread_c(engine):
            empty(gamma_beta[:], spread_bank[0][:], engine)

        sgn_sin = one.tile([P, NT, HALF, 2], BF16, name="sgn_sin")

        def signed_sin():
            for j, sign in enumerate((-1.0, 1.0)):
                nc.gpsimd.tensor_scalar(
                    out=sgn_sin[:, :, :, j], in0=sin[:], scalar1=sign, scalar2=0.0, op0=ALU.mult, op1=ALU.add
                )

        wa_codes = [one.tile([P, KV], U32, name=f"wa_codes{g}", align_bytes=64) for g in range(NG)]
        wa_scales = [one.tile([P, KV], U8, name=f"wa_scales{g}", align_bytes=64) for g in range(NG)]
        hid_codes = [one.tile([P, NG * P], U32, name=f"hid_codes{i}", align_bytes=64) for i in range(NT)]
        hid_scales = [one.tile([P, NG * P], U8, name=f"hid_scales{i}", align_bytes=64) for i in range(NT)]

        wa_grouped = [one.tile([P, KV, PACK], BF16, name=f"wa_grouped{g}", align_bytes=64) for g in range(NG)]

        def wa_i(g, a, b, engine):
            dst = wa_grouped[g][:, a:b, :].rearrange("p (c i) t -> p c t i", i=4)
            src = wa_raw[g][:, :, a:b].rearrange("p t (c i) -> p c t i", i=4)
            if engine == "v":
                nc.vector.tensor_copy(out=dst, in_=src)
            else:
                nc.scalar.copy(out=dst, in_=src)

        wa_bank = {}

        def wa_m(g, j):
            bank = psum.tile([P, 256, PACK], BF16, name="bank", tag="bank")
            for m in range(2):
                c0 = 256 * j + P * m
                nc.tensor.matmul(
                    bank[:, P * m : P * (m + 1), :].rearrange("p c t -> p t c"),
                    lhsT=ident_bf[:],
                    rhs=wa_raw[g][:, :, c0 : c0 + P],
                    start=True,
                    stop=True,
                )
            wa_bank[g, j] = bank

        def wa_e(g, j, engine):
            out = wa_grouped[g][:, 256 * j : 256 * (j + 1), :].rearrange("p c t -> p (c t)")
            empty(out, wa_bank[g, j][:].rearrange("p c t -> p (c t)"), engine)

        def wa_q(g, a, b):
            flat = wa_grouped[g][:].rearrange("p c t -> p (c t)")
            nc.vector.quantize_mx(
                out=wa_codes[g][:, a:b].bitcast(FP8X4), scales=wa_scales[g][:, a:b], in_=flat[:, a * PACK : b * PACK]
            )

        hid_grouped = [one.tile([P, NG * P * PACK], BF16, name=f"hid_grouped{i}", align_bytes=64) for i in range(NT)]

        hid_bank = {}

        def hid_t(i, half):
            words = hid[i][:].bitcast(F32)
            xt = psum.tile([P, 2, 2, P], F32, name="bank", tag="bank")
            for gg in range(2):
                g = 2 * half + gg
                for u in range(2):
                    nc.tensor.transpose(xt[:, gg, u, :], words[:, 256 * g + u : 256 * (g + 1) : 2], ident[:])
            hid_bank[i, half] = xt

        def hid_c(i, half, engine):
            out = hid_grouped[i][:, half * 1024 : (half + 1) * 1024].bitcast(F32).rearrange("p (g r u) -> p g r u", g=2, u=2)
            empty(out, hid_bank[i, half][:].rearrange("p g u r -> p g r u"), engine)

        def hid_q(i):
            nc.vector.quantize_mx(out=hid_codes[i][:].bitcast(FP8X4), scales=hid_scales[i][:], in_=hid_grouped[i][:])

        kv = {}
        rp = {}

        def mm1(dst, i, g, a, b):
            toks = slice(g * P, (g + 1) * P)
            nc.tensor.matmul_mx(
                out=dst,
                lhsT=hid_codes[i][:, toks].bitcast(FP8X4),
                lhsT_scale=hid_scales[i][:, toks],
                rhs=wa_codes[g][:, a:b].bitcast(FP8X4),
                rhs_scale=wa_scales[g][:, a:b],
                start=(g == 0),
                stop=(g == NG - 1),
            )

        def mml(i, g):
            if g == 0:
                bank = psum.tile([P, LAT], F32, name="bank", tag="bank")
                kv[i] = bank
            mm1(kv[i][:], i, g, 0, LAT)

        def mmr(i, g):
            if g == 0:
                bank = psum.tile([P, 512], F32, name="bank", tag="bank")
                rp[i] = bank
            mm1(rp[i][:, 0:ROPE], i, g, LAT, KV)

        lat = {}
        k_sb = {}
        for i in range(DIRECT, NT):
            k_sb[i, 0] = one.tile([P, 2 * GH, NOPE + ROPE], F32, name=f"k_sb{i}", align_bytes=64)
            k_sb[i, 1] = k_sb[i, 0]
        k_sb[NT - 1, 1] = one.tile([P, 2 * GH, NOPE + ROPE], F32, name="k_sb_last", align_bytes=64)

        mvs = {}
        rstds = {}
        cens = {}

        stats = {}

        def bn_s(i):
            stat = work.tile([P, 6], F32, name="stat", bufs=4)
            nc.vector.bn_stats(out=stat[:], in_=kv[i][:])
            stats[i] = stat

        def bn_a(i):
            mv = work.tile([P, 2], F32, name="mv", bufs=4)
            nc.vector.bn_aggr(out=mv[:], in_=stats[i][:])
            ve = work.tile([P, 1], F32, name="ve", bufs=4)
            rstd = work.tile([P, 1], F32, name="rstd", bufs=4)
            nc.gpsimd.tensor_scalar(out=ve[:], in0=mv[:, 1:2], scalar1=EPS, scalar2=None, op0=ALU.add)
            nc.gpsimd.tensor_tensor(out=rstd[:], in0=ve[:], in1=neg_half[:], op=ALU.pow)
            mvs[i] = mv
            rstds[i] = rstd

        def cen(i):
            cens[i] = work.tile([P, LAT], F32, name="cen", bufs=2)
            nc.vector.scalar_tensor_tensor(
                out=cens[i][:], in0=kv[i][:], scalar=mvs[i][:, 0:1], in1=gamma, op0=ALU.subtract, op1=ALU.mult
            )

        def fin(i):
            lat[i] = work.tile([P, LAT], BF16, name="lat", bufs=4, align_bytes=64)
            nc.vector.scalar_tensor_tensor(
                out=lat[i][:], in0=cens[i][:], scalar=rstds[i][:], in1=beta, op0=ALU.mult, op1=ALU.add
            )

        rots = {}

        def rope_a(i):
            x = rp[i][:, 0:ROPE].rearrange("p (c two) -> p c two", two=2)
            xc = work.tile([P, HALF, 2], F32, name="xc", bufs=2)
            xs = work.tile([P, HALF, 2], F32, name="xs", bufs=2)
            rots[i] = (xc, xs)
            c2 = cos[:, i, :].unsqueeze(2).to_broadcast([P, HALF, 2])
            nc.vector.tensor_tensor(out=xc[:], in0=x, in1=c2, op=ALU.mult)
            nc.vector.tensor_tensor(out=xs[:], in0=x[:, :, ::-1], in1=sgn_sin[:, i], op=ALU.mult)

        def rope_b(i):
            xc, xs = rots[i]
            r = work.tile([P, ROPE], F32, name="r", bufs=4)
            nc.vector.tensor_tensor(
                out=r[:].rearrange("p (c two) -> p c two", two=2), in0=xc[:], in1=xs[:], op=ALU.add
            )
            rots[i] = r

        def rope_d(i):
            nc.sync.dma_start(out=k_v[i][:, :, NOPE:], in_=rots[i][:].unsqueeze(1).to_broadcast([P, H, ROPE]))

        def rope_r(i, h, a, b, engine):
            copies = rots[i][:].unsqueeze(1).to_broadcast([P, (b - a) * GH, ROPE])
            empty(k_sb[i, h][:, a * GH : b * GH, NOPE:], copies, engine)

        lat_codes = [one.tile([P, P], U32, name=f"lat_codes{i}", align_bytes=64) for i in range(NT)]
        lat_scales = [one.tile([P, P], U8, name=f"lat_scales{i}", align_bytes=64) for i in range(NT)]

        lat_grouped = [one.tile([P, P * PACK], BF16, name=f"lat_grouped{i}", align_bytes=64) for i in range(NT)]

        lat_bank = {}

        def lat_t(i):
            words = lat[i][:].bitcast(F32)
            xt = psum.tile([P, 4, P], F32, name="bank", tag="bank")
            for u in range(2):
                nc.tensor.transpose(xt[:, u, :], words[:, u::2], ident[:])
            lat_bank[i] = xt

        def lat_c(i, engine):
            out = lat_grouped[i][:].bitcast(F32).rearrange("p (r u) -> p r u", u=2)
            empty(out, lat_bank[i][:, 0:2, :].rearrange("p u r -> p r u"), engine)

        def lat_q(i):
            nc.vector.quantize_mx(out=lat_codes[i][:].bitcast(FP8X4), scales=lat_scales[i][:], in_=lat_grouped[i][:])

        v_codes = [one.tile([P, GV], U32, name=f"v_codes{q}", align_bytes=64) for q in range(NHG)]
        v_scales = [one.tile([P, GV], U8, name=f"v_scales{q}", align_bytes=64) for q in range(NHG)]
        n_codes = [one.tile([P, 2 * GN], U32, name=f"n_codes{h}", align_bytes=64) for h in range(NHG // 2)]
        n_scales = [one.tile([P, 2 * GN], U8, name=f"n_scales{h}", align_bytes=64) for h in range(NHG // 2)]

        wide = {}
        gvs = {}
        gns = {}

        def wb_w(h, t, a, b):
            if h not in wide:
                wide[h] = work.tile([P, PACK // 2, 2 * GC, 2], BF16, name="wb_wide", align_bytes=64)
            raw = wb_bytes[t][:, (2 * h + a) * GC : (2 * h + b) * GC].bitcast(FP8)
            nc.vector.tensor_scalar(
                out=wide[h][:, t // 2, a * GC : b * GC, t % 2], in0=raw, scalar1=wb_scale[:, t : t + 1], scalar2=None, op0=ALU.mult
            )

        def wide_words(h):
            words = wide[h][:].rearrange("p u n e -> p u (n e)").bitcast(F32)
            return words.rearrange("p u (h c) -> p h c u", h=2 * GH)

        def word_view(grouped):
            words = grouped.rearrange("p h c t -> p h (c t)").bitcast(F32)
            return words.rearrange("p h (c u) -> p h c u", u=2)

        def wb_iv(q, part, engine):
            if q not in gvs:
                gvs[q] = work.tile([P, GH, VD, PACK], BF16, name="wb_gv", align_bytes=64)
            first = (q % 2) * GH + part * GH // 2
            empty(
                word_view(gvs[q][:, part * GH // 2 : (part + 1) * GH // 2]),
                wide_words(q // 2)[:, first : first + GH // 2, NOPE:],
                engine,
            )

        def wb_in(h, part, engine):
            if h not in gns:
                gns[h] = work.tile([P, 2 * GH, NOPE, PACK], BF16, name="wb_gn", align_bytes=64)
            some = slice(part * GH, (part + 1) * GH)
            empty(word_view(gns[h][:, some]), wide_words(h)[:, some, :NOPE], engine)

        def wb_qv(q):
            nc.vector.quantize_mx(
                out=v_codes[q][:].bitcast(FP8X4), scales=v_scales[q][:], in_=gvs[q][:].rearrange("p h c t -> p (h c t)")
            )

        def wb_qn(h, a, b):
            nc.vector.quantize_mx(
                out=n_codes[h][:, a * GN : b * GN].bitcast(FP8X4),
                scales=n_scales[h][:, a * GN : b * GN],
                in_=gns[h][:, a * GH : b * GH].rearrange("p h c t -> p (h c t)"),
            )

        banks = {}

        def mm2(key, i, codes, scales, n=512):
            bank = psum.tile([P, 512], F32, name="bank", tag="bank")
            nc.tensor.matmul_mx(
                out=bank[:, 0:n],
                lhsT=lat_codes[i][:].bitcast(FP8X4),
                lhsT_scale=lat_scales[i][:],
                rhs=codes.bitcast(FP8X4),
                rhs_scale=scales,
                start=True,
                stop=True,
            )
            banks[key] = bank

        def mv(i, q):
            mm2(("v", i, q), i, v_codes[q][:], v_scales[q][:])

        def mk(i, h, a, b):
            cols = slice(a * GN, b * GN)
            mm2(("k", i, h, a), i, n_codes[h][:, cols], n_scales[h][:, cols], (b - a) * GN)

        v_out = {}

        def ov(i, q, engine):
            if (i, q // 2) not in v_out:
                v_sb = work.tile([P, 2 * GV], F32, name="v_sb", bufs=4)
                v_out[i, q // 2] = v_sb
            half = slice((q % 2) * GV, (q % 2 + 1) * GV)
            empty(v_out[i, q // 2][:, half], banks["v", i, q][:], engine)

        def sv(i, h, a, b):
            nc.sync.dma_start(out=v_v[i][:, (2 * h + a) * GV : (2 * h + b) * GV], in_=v_out[i, h][:, a * GV : b * GV])

        n_out = {}

        def ok(i, h, a, b, engine):
            keys = banks["k", i, h, a][:, 0 : (b - a) * GN].rearrange("p (h c) -> p h c", c=NOPE)
            if i < DIRECT:
                n_sb = work.tile([P, 2 * GH, NOPE], F32, name="n_sb", bufs=3)
                n_out[i, h] = n_sb
                empty(n_sb[:], keys, engine)
            else:
                empty(k_sb[i, h][:, a * GH : b * GH, :NOPE], keys, engine)

        def sk(i, h, a, b):
            heads = slice((2 * h + a) * GH, (2 * h + b) * GH)
            if i < DIRECT:
                nc.sync.dma_start(out=k_v[i][:, heads, :NOPE], in_=n_out[i, h][:])
            else:
                nc.sync.dma_start(out=k_v[i][:, heads, :], in_=k_sb[i, h][:, a * GH : b * GH, :])

        with tc.manual_schedule():
            load_wb(0, 2, 4)
            load_wb(2, 0, 2)
            load_gb()
            load_wa(1)
            wa_i(1, 512, 640, "s")
            load_wb(1, 2, 4)
            wb_w(1, 0, 0, 2)
            wb_w(0, 2, 0, 2)
            spread_m()
            spread_c("s")
            wa_m(1, 1)
            load_wb(2, 2, 4)
            wb_w(1, 1, 0, 2)
            wb_w(1, 2, 0, 2)
            load_wb(3, 2, 4)
            load_wa(2)
            wa_m(1, 0)
            wa_m(2, 0)
            wa_e(1, 1, "s")
            wa_m(2, 1)
            wa_i(2, 512, 640, "s")
            load_wa(0)
            load_wb(0, 0, 2)
            load_hid(3)
            wa_e(1, 0, "s")
            wb_w(1, 3, 0, 2)
            wa_q(1, 0, 512)
            wb_in(1, 1, "v")
            wa_i(0, 512, 640, "s")
            load_wb(3, 0, 2)
            hid_t(3, 1)
            wb_w(0, 0, 0, 2)
            wb_w(0, 3, 0, 2)
            wb_iv(3, 0, "s")
            wb_iv(3, 1, "s")
            wa_e(2, 0, "s")
            load_rot()
            wa_e(2, 1, "s")
            wa_m(0, 1)
            wb_in(1, 0, "s")
            hid_c(3, 1, "s")
            load_wa(3)
            wa_m(0, 0)
            wb_qv(3)
            wa_q(1, 512, 640)
            wa_q(2, 512, 640)
            wa_e(0, 1, "s")
            hid_t(3, 0)
            wa_q(2, 0, 512)
            load_wb(1, 0, 2)
            wa_i(3, 512, 640, "v")
            wa_q(0, 512, 640)
            wb_w(0, 1, 0, 2)
            wa_i(3, 256, 512, "s")
            signed_sin()
            wa_q(3, 512, 640)
            load_hid(2)
            wa_m(3, 0)
            hid_c(3, 0, "s")
            hid_q(3)
            load_hid(0)
            wa_e(0, 0, "s")
            wa_e(3, 0, "s")
            hid_t(0, 0)
            hid_t(0, 1)
            wa_q(0, 0, 512)
            mmr(3, 0)
            mml(3, 0)
            mml(3, 1)
            mml(3, 2)
            wb_qn(1, 0, 2)
            hid_c(0, 0, "s")
            mmr(3, 1)
            wa_q(3, 0, 512)
            hid_c(0, 1, "s")
            hid_q(0)
            load_hid(1)
            mmr(3, 2)
            mmr(3, 3)
            mml(3, 3)
            mmr(0, 0)
            rope_a(3)
            wb_iv(0, 0, "s")
            wb_iv(2, 0, "s")
            mmr(0, 1)
            mmr(0, 2)
            mmr(0, 3)
            wb_iv(2, 1, "s")
            bn_s(3)
            rope_b(3)
            hid_t(1, 0)
            bn_a(3)
            rope_a(0)
            wb_in(0, 0, "s")
            cen(3)
            hid_c(1, 0, "s")
            hid_t(1, 1)
            mml(0, 0)
            hid_c(1, 1, "s")
            mml(0, 1)
            mml(0, 2)
            rope_b(0)
            fin(3)
            hid_q(1)
            mml(0, 3)
            bn_s(0)
            lat_t(3)
            rope_r(3, 0, 0, 2, "s")
            lat_c(3, "s")
            hid_t(2, 0)
            wb_in(0, 1, "v")
            rope_d(0)
            bn_a(0)
            mml(1, 0)
            mml(1, 1)
            rope_r(3, 1, 0, 2, "s")
            lat_q(3)
            mk(3, 1, 0, 2)
            ok(3, 1, 0, 2, "s")
            cen(0)
            wb_qn(0, 0, 2)
            mml(1, 2)
            mml(1, 3)
            hid_c(2, 0, "s")
            mk(3, 0, 0, 2)
            mmr(1, 0)
            fin(0)
            mmr(1, 1)
            mmr(1, 2)
            lat_t(0)
            ok(3, 0, 0, 2, "s")
            sk(3, 1, 0, 2)
            mv(3, 3)
            wb_iv(0, 1, "s")
            mmr(1, 3)
            wb_qv(2)
            mv(3, 2)
            bn_s(1)
            hid_t(2, 1)
            ov(3, 3, "s")
            lat_c(0, "v")
            bn_a(1)
            ov(3, 2, "s")
            lat_q(0)
            hid_c(2, 1, "s")
            mk(0, 0, 0, 2)
            ok(0, 0, 0, 2, "s")
            mk(0, 1, 0, 2)
            cen(1)
            mv(0, 2)
            rope_a(1)
            mv(0, 3)
            fin(1)
            lat_t(1)
            hid_q(2)
            ov(0, 2, "v")
            mml(2, 0)
            mml(2, 1)
            mml(2, 2)
            rope_b(1)
            ok(0, 1, 0, 2, "s")
            sk(3, 0, 0, 2)
            ov(0, 3, "s")
            sv(3, 1, 0, 2)
            wb_qv(0)
            lat_c(1, "s")
            wb_iv(1, 0, "s")
            lat_q(1)
            mml(2, 3)
            wb_iv(1, 1, "s")
            mmr(2, 0)
            mk(1, 0, 0, 2)
            sk(0, 0, 0, 2)
            mv(1, 3)
            mmr(2, 1)
            mv(3, 0)
            rope_r(1, 0, 0, 2, "v")
            bn_s(2)
            wb_qv(1)
            mv(1, 2)
            ok(1, 0, 0, 2, "s")
            mv(3, 1)
            ov(1, 3, "s")
            mmr(2, 2)
            ov(1, 2, "s")
            ov(3, 1, "s")
            bn_a(2)
            ov(3, 0, "v")
            mv(1, 1)
            ov(1, 1, "s")
            mv(0, 1)
            cen(2)
            mv(1, 0)
            fin(2)
            mk(1, 1, 0, 2)
            sk(0, 1, 0, 2)
            mmr(2, 3)
            ov(1, 0, "s")
            sv(0, 1, 0, 2)
            rope_a(2)
            lat_t(2)
            lat_c(2, "v")
            rope_b(2)
            mv(0, 0)
            lat_q(2)
            mk(2, 0, 0, 2)
            sk(1, 0, 0, 2)
            ok(1, 1, 0, 2, "s")
            mv(2, 0)
            ov(0, 0, "v")
            sv(1, 1, 0, 2)
            rope_r(2, 0, 0, 2, "v")
            sv(3, 0, 0, 2)
            ov(0, 1, "s")
            mv(2, 1)
            ov(2, 1, "v")
            mv(2, 2)
            sv(1, 0, 0, 2)
            ok(2, 0, 0, 2, "s")
            ov(2, 0, "s")
            sk(1, 1, 0, 2)
            mv(2, 3)
            sk(2, 0, 0, 2)
            ov(2, 2, "s")
            mk(2, 1, 0, 2)
            ok(2, 1, 0, 2, "s")
            ov(2, 3, "v")
            sv(0, 0, 0, 2)
            sv(2, 0, 0, 2)
            sv(2, 1, 0, 2)
            sk(2, 1, 0, 2)
